import numpy as np
import ml_dtypes


def mxq(x, axis, fmt="e4m3"):
    dtype, down = {"e4m3": (ml_dtypes.float8_e4m3fn, 7), "e5m2": (ml_dtypes.float8_e5m2, 14)}[fmt]
    v = np.moveaxis(np.asarray(x, np.float32).astype(ml_dtypes.bfloat16).astype(np.float64), axis, -1)
    blocks = v.reshape(v.shape[:-1] + (-1, 32))
    amax = np.abs(blocks).max(-1, keepdims=True)
    byte = np.maximum(np.where(amax > 0, np.frexp(amax)[1] - 1 + 127, 0) - down, 1)
    scale = np.exp2(byte - 127.0)
    codes = (blocks / scale).astype(np.float32).astype(dtype).astype(np.float64)
    return np.moveaxis((codes * scale).reshape(v.shape), -1, axis)


WIDE = False


def mx_kscale(k):
    if not WIDE:
        return np.ones(k)
    levels = np.array([10, -10, 5, -5, 0])
    a = np.random.permutation(np.resize(levels, k // 512 * 4)).reshape(k // 512, 4)
    idx = np.arange(k)
    return np.exp2(a[idx // 512, idx % 128 // 32])


BF16 = ml_dtypes.bfloat16


def bf(x):
    return np.asarray(x, np.float32).astype(BF16)


def f64(x):
    return np.asarray(x).astype(np.float64)


E2M1 = np.array([0.0, 0.5, 1.0, 1.5, 2.0, 3.0, 4.0, 6.0, -0.0, -0.5, -1.0, -1.5, -2.0, -3.0, -4.0, -6.0])


def pack_weight(w, fmt):
    k, n = w.shape
    w = f64(bf(w)).reshape(k // 32, 32, n)
    amax = np.abs(w).max(1)
    if fmt == "e4m3":
        byte = np.frexp(amax)[1] - 1 + 127 - 7
    else:
        mant, ex = np.frexp(amax / 6.0)
        byte = np.where(mant > 0.5, ex, ex - 1) + 127
    byte = np.clip(np.where(amax > 0, byte, 1), 1, 254)
    scaled = (w * np.exp2(127.0 - byte)[:, None, :]).reshape(k, n).astype(np.float32)
    by_word = np.ascontiguousarray(scaled.reshape(k // 512, 128, 4, n).transpose(0, 1, 3, 2))
    if fmt == "e4m3":
        words = by_word.astype(ml_dtypes.float8_e4m3fn).view(np.uint8)
    else:
        c = by_word.astype(ml_dtypes.float4_e2m1fn).view(np.uint8) & 0xF
        words = c[..., 0::2] | (c[..., 1::2] << 4)
    return np.ascontiguousarray(words), np.ascontiguousarray(byte.astype(np.uint8).reshape(k // 512, 16, n))


def unpack_weight(words, scales, fmt):
    g, p, n, _ = words.shape
    if fmt == "e4m3":
        vals = np.ascontiguousarray(words).view(ml_dtypes.float8_e4m3fn).astype(np.float64)
    else:
        nib = np.empty((g, p, n, 4), np.uint8)
        nib[..., 0::2] = words & 0xF
        nib[..., 1::2] = words >> 4
        vals = E2M1[nib]
    vals = vals * np.repeat(np.exp2(scales.astype(np.float64) - 127.0), 8, axis=1)[..., None]
    return vals.transpose(0, 1, 3, 2).reshape(g * 512, n)

def pack4(w):
    words, scales = pack_weight(w, "e2m1")
    return words.reshape(words.shape[0], 128, -1), scales


def unpack4(words, scales):
    return unpack_weight(words.reshape(words.shape[0], 128, -1, 2), scales, "e2m1")


B, N, D1, D2, NS = 512, 8, 512, 256, 2
ND = D1
NP = N // NS


def rolled_concat(arrays, n, axis=-1):
    return np.concatenate(arrays[n:] + arrays[:n], axis=axis)


def setup_inputs():
    t = mx_kscale(NS * D2)
    tb = t.reshape(NS, D2)
    fac = np.stack([np.roll(tb, i, axis=0) for i in range(NS)])
    x2 = np.random.standard_normal((B, NS, NP, NS, NP, D2)) * fac[None, :, None, :, None, :]
    in_1e = bf(np.random.standard_normal((B, N, D1)))
    in_2e = bf(x2.reshape(B, N, N, D2))
    wu_words, wu_scales = pack4(np.random.standard_normal((D1, ND)) * 0.6 / np.sqrt(D1))
    b_unmixed = bf(np.random.standard_normal(ND) * 0.3)
    wm_words, wm_scales = pack4(np.random.standard_normal((NS * D1, ND)) * 0.6 * np.sqrt(NP) / np.sqrt(NS * D1))
    w2_words, w2_scales = pack4(np.random.standard_normal((NS * D2, ND)) * 0.6 * np.sqrt(NP) / np.sqrt(NS * D2) / t[:, None])
    return {"in_1e": in_1e,
            "in_2e": in_2e,
            "W_unmixed_words": wu_words,
            "W_unmixed_scales": wu_scales,
            "b_unmixed": b_unmixed,
            "W_mixed_words": wm_words,
            "W_mixed_scales": wm_scales,
            "W_2e_words": w2_words,
            "W_2e_scales": w2_scales}


def reference(in_1e, in_2e, W_unmixed_words, W_unmixed_scales, b_unmixed, W_mixed_words, W_mixed_scales, W_2e_words, W_2e_scales):
    x1, x2 = f64(in_1e), f64(in_2e)
    dense_unmixed = (mxq(x1, 2, "e4m3") @ unpack4(W_unmixed_words, W_unmixed_scales)) + f64(b_unmixed)
    split_unmixed = np.split(dense_unmixed, NS, axis=-2)
    split_1e = np.split(x1, NS, axis=-2)
    split_means = [np.mean(s, axis=-2, keepdims=True) for s in split_1e]
    split_concat = [rolled_concat(split_means, i) for i in range(NS)]
    all_spins = np.concatenate(split_concat, axis=-2)
    dense_mixed = mxq(all_spins, 2, "e4m3") @ unpack4(W_mixed_words, W_mixed_scales)
    dense_mixed_split = np.split(dense_mixed, NS, axis=-2)
    split_2e = np.split(x2, NS, axis=-3)
    concat_2e = []
    for spin in range(NS):
        blocks = np.split(split_2e[spin], NS, axis=-2)
        means = [np.mean(p, axis=-2) for p in blocks]
        concat_2e.append(rolled_concat(means, spin))
    all_2e = np.concatenate(concat_2e, axis=-2)
    dense_2e = mxq(all_2e, 2, "e4m3") @ unpack4(W_2e_words, W_2e_scales)
    dense_2e_split = np.split(dense_2e, NS, axis=-2)
    out_splits = [u + m + e for u, m, e in zip(split_unmixed, dense_mixed_split, dense_2e_split)]
    dense_out = np.concatenate(out_splits, axis=-2)
    return np.tanh(dense_out) + x1

@@ -1,0 +1,226 @@
+from contextlib import ExitStack
+
+import concourse.mybir as mybir
+from concourse.masks import make_identity
+
+F32 = mybir.dt.float32
+BF16 = mybir.dt.bfloat16
+I32 = mybir.dt.int32
+U32 = mybir.dt.uint32
+U8 = mybir.dt.uint8
+FP8X4 = mybir.dt.float8_e4m3fn_x4
+FP4X4 = mybir.dt.float4_e2m1fn_x4
+ADD = mybir.AluOpType.add
+ACT = mybir.ActivationFunctionType
+
+P = 128
+WALKERS = 512
+SPINS = 2
+PER_SPIN = 4
+D1 = 512
+D2 = 256
+PACK = 4
+BLOCKS = WALKERS // P
+GROUPS = BLOCKS * SPINS
+PAIRS = PER_SPIN // 2
+
+W_U, W_M_OWN, W_M_OTHER, W_E = 0, 1, 2, 3
+N_PASSES = 4
+
+FLOPS = 2 * WALKERS * 8 * D1 * D1 * 2 + 2 * WALKERS * SPINS * (SPINS * D1) * D1
+
+
+def tile_ferminetoneelectronlayer_pa_t_kernel(
+    tc, in_1e, in_2e, wu_words, wu_scales, b_unmixed, wm_words, wm_scales, w2_words, w2_scales, out
+):
+    nc = tc.nc
+    with ExitStack() as ctx:
+        const = ctx.enter_context(tc.tile_pool(name="const", bufs=1))
+        x1_pool = ctx.enter_context(tc.tile_pool(name="x1", bufs=3))
+        e2_pool = ctx.enter_context(tc.tile_pool(name="e2", bufs=2 * PAIRS))
+        work = ctx.enter_context(tc.tile_pool(name="work", bufs=2))
+        out_pool = ctx.enter_context(tc.tile_pool(name="o", bufs=3))
+        tp_pool = ctx.enter_context(tc.psum_pool(name="tp", bufs=4))
+        acc_pool = ctx.enter_context(tc.psum_pool(name="acc", bufs=4))
+
+        planes = const.tile([P, N_PASSES, D1], U8, align_bytes=64)
+        nc.vector.memset(planes[:].rearrange("p w n -> p (w n)").bitcast(I32), 0)
+        words = const.tile([P, N_PASSES, 2 * D1], U8, align_bytes=64)
+        bias_bc = const.tile([P, D1], BF16)
+        ident = const.tile([P, P], F32)
+        make_identity(nc, ident[:])
+
+        def load_weight(place, w_words, w_scales):
+            last = place + w_words.shape[0]
+            nc.sync.dma_start(
+                out=words[:, place:last, :].bitcast(I32), in_=w_words.rearrange("g p n -> p g n").bitcast(I32)
+            )
+            for quad in range(4):
+                nc.sync.dma_start(
+                    out=planes[32 * quad : 32 * quad + 4, place:last, :].bitcast(I32),
+                    in_=w_scales[:, 4 * quad : 4 * quad + 4, :].rearrange("g r n -> r g n").bitcast(I32),
+                )
+
+        x1_of, e2_of, sums_of, grouped_of, codes_of, gb_of, o_of = {}, {}, {}, {}, {}, {}, {}
+
+        def load_group(n):
+            blk, spin = divmod(n, SPINS)
+            walkers = slice(blk * P, (blk + 1) * P)
+            if spin == 0:
+                x1 = x1_pool.tile([P, SPINS * PER_SPIN, D1], BF16)
+                nc.sync.dma_start(out=x1[:], in_=in_1e[walkers])
+                x1_of[blk] = x1
+            for pair in range(PAIRS):
+                e2 = e2_pool.tile([P, 2, SPINS, PER_SPIN, D2], BF16)
+                first = spin * PER_SPIN + 2 * pair
+                for h in range(SPINS):
+                    partner = ((spin + h) % SPINS) * PER_SPIN
+                    nc.sync.dma_start(
+                        out=e2[:, :, h, :, :], in_=in_2e[walkers, first : first + 2, partner : partner + PER_SPIN, :]
+                    )
+                e2_of[n, pair] = e2
+
+        def sum_one_electron(blk):
+            halves = x1_of[blk][:].rearrange("p (s h l) d -> p s h (l d)", s=SPINS, h=2, l=2)
+            m_half = work.tile([P, SPINS, 2 * D1], F32, bufs=1)
+            nc.vector.tensor_tensor(out=m_half[:], in0=halves[:, :, 0, :], in1=halves[:, :, 1, :], op=ADD)
+            m_sum = work.tile([P, SPINS, D1], BF16)
+            rest = m_half[:].rearrange("p s (l d) -> p s l d", l=2)
+            nc.vector.tensor_tensor(out=m_sum[:], in0=rest[:, :, 0, :], in1=rest[:, :, 1, :], op=ADD)
+            sums_of["m", blk] = m_sum
+
+        def sum_two_electron(n, pair):
+            if pair == 0:
+                a_sum = work.tile([P, PER_SPIN, SPINS * D2], BF16)
+                sums_of["a", n] = a_sum
+            a_sum = sums_of["a", n]
+            halves = e2_of[n, pair][:].rearrange("p i s (h l) d -> p (i s) h (l d)", h=2, l=2)
+            a_half = work.tile([P, 2 * SPINS, 2 * D2], F32)
+            nc.vector.tensor_tensor(out=a_half[:], in0=halves[:, :, 0, :], in1=halves[:, :, 1, :], op=ADD)
+            rest = a_half[:].rearrange("p g (l d) -> p g l d", l=2)
+            nc.vector.tensor_tensor(
+                out=a_sum[:, 2 * pair : 2 * pair + 2, :].rearrange("p i (s d) -> p (i s) d", s=SPINS),
+                in0=rest[:, :, 0, :],
+                in1=rest[:, :, 1, :],
+                op=ADD,
+            )
+
+        def transpose_rows(rows, count):
+            as_words = rows.bitcast(F32)
+            banks = []
+            for first in range(0, count, 2):
+                bank = tp_pool.tile([P, 2 * 2, P], F32, tag="tp")
+                for r in range(2):
+                    for u in range(2):
+                        nc.tensor.transpose(bank[:, 2 * r + u, :], as_words[:, first + r, u : D1 // 2 : 2], ident[:])
+                banks.append(bank)
+            return banks
+
+        def copy_scaled(grouped, banks):
+            for b, bank in enumerate(banks):
+                values = bank[:].rearrange("p a w -> p (a w)").bitcast(BF16)
+                values = values.rearrange("p (r u w e) -> p r w u e", r=2, u=2, w=P, e=2)
+                for r in range(2):
+                    nc.scalar.activation(
+                        out=grouped[:, 2 * b + r, :, :].rearrange("p w (u e) -> p w u e", u=2),
+                        in_=values[:, r],
+                        func=ACT.Copy,
+                        scale=1.0 / PER_SPIN,
+                    )
+
+        def transpose_group(n):
+            blk, spin = divmod(n, SPINS)
+            x_banks = transpose_rows(x1_of[blk][:, spin * PER_SPIN : (spin + 1) * PER_SPIN, :], PER_SPIN)
+            x_grouped = work.tile([P, PER_SPIN, P, PACK], BF16, align_bytes=64)
+            x_words = x_grouped[:].rearrange("p i w t -> p (i w t)").bitcast(F32)
+            x_words = x_words.rearrange("p (i w u) -> p i w u", i=PER_SPIN, w=P, u=2)
+            for b, bank in enumerate(x_banks):
+                nc.scalar.copy(out=x_words[:, 2 * b : 2 * b + 2], in_=bank[:].rearrange("p (r u) w -> p r w u", u=2))
+            grouped_of["x", n] = x_grouped
+            if spin == 0:
+                m_banks = transpose_rows(sums_of["m", blk][:], SPINS)
+                m_grouped = work.tile([P, SPINS, P, PACK], BF16, align_bytes=64)
+                copy_scaled(m_grouped, m_banks)
+                grouped_of["m", blk] = m_grouped
+            a_banks = transpose_rows(sums_of["a", n][:], PER_SPIN)
+            a_grouped = work.tile([P, PER_SPIN, P, PACK], BF16, align_bytes=64)
+            copy_scaled(a_grouped, a_banks)
+            grouped_of["a", n] = a_grouped
+
+        def quantise(key, count):
+            grouped = grouped_of[key]
+            codes = work.tile([P, count, P], U32, align_bytes=64, tag="codes_" + key[0])
+            scales = work.tile([P, count, P], U8, align_bytes=64, tag="scales_" + key[0])
+            nc.vector.quantize_mx(
+                out=codes[:].rearrange("p i w -> p (i w)").bitcast(FP8X4),
+                scales=scales[:].rearrange("p i w -> p (i w)"),
+                in_=grouped[:].rearrange("p i w t -> p (i w t)"),
+            )
+            codes_of[key] = (codes, scales)
+
+        def quantise_group(n):
+            blk, spin = divmod(n, SPINS)
+            quantise(("x", n), PER_SPIN)
+            if spin == 0:
+                quantise(("m", blk), SPINS)
+            quantise(("a", n), PER_SPIN)
+
+        def mx_pass(acc, key, row, place, start, stop):
+            codes, scales = codes_of[key]
+            nc.tensor.matmul_mx(
+                out=acc[:],
+                lhsT=codes[:, row, :].bitcast(FP8X4),
+                lhsT_scale=scales[:, row, :],
+                rhs=words[:, place, :].bitcast(FP4X4),
+                rhs_scale=planes[:, place, :],
+                start=start,
+                stop=stop,
+            )
+
+        def multiply_group(n):
+            blk, spin = divmod(n, SPINS)
+            if spin == 0:
+                gb = work.tile([P, SPINS, D1], F32)
+                for s in range(SPINS):
+                    acc_g = acc_pool.tile([P, D1], F32, tag="acc")
+                    mx_pass(acc_g, ("m", blk), s, W_M_OWN, True, False)
+                    mx_pass(acc_g, ("m", blk), 1 - s, W_M_OTHER, False, True)
+                    nc.vector.tensor_tensor(out=gb[:, s, :], in0=acc_g[:], in1=bias_bc[:], op=ADD)
+                gb_of[blk] = gb
+            o = out_pool.tile([P, PER_SPIN, D1], F32)
+            for i in range(PER_SPIN):
+                acc = acc_pool.tile([P, D1], F32, tag="acc")
+                mx_pass(acc, ("x", n), i, W_U, True, False)
+                mx_pass(acc, ("a", n), i, W_E, False, True)
+                nc.vector.tensor_tensor(out=o[:, i, :], in0=acc[:], in1=gb_of[blk][:, spin, :], op=ADD)
+            nc.scalar.activation(out=o[:], in_=o[:], func=ACT.Tanh)
+            o_of[n] = o
+
+        def finish_group(n):
+            blk, spin = divmod(n, SPINS)
+            electrons = slice(spin * PER_SPIN, (spin + 1) * PER_SPIN)
+            o = o_of[n]
+            nc.vector.tensor_tensor(out=o[:], in0=o[:], in1=x1_of[blk][:, electrons, :], op=ADD)
+            nc.sync.dma_start(out=out[blk * P : (blk + 1) * P, electrons, :], in_=o[:])
+
+        load_group(0)
+        load_weight(W_U, wu_words, wu_scales)
+        load_weight(W_M_OWN, wm_words, wm_scales)
+        load_weight(W_E, w2_words, w2_scales)
+        nc.sync.dma_start(out=bias_bc[:], in_=b_unmixed.partition_broadcast(P))
+        for n in range(GROUPS + 1):
+            if n + 1 < GROUPS:
+                load_group(n + 1)
+            if n > 0:
+                quantise_group(n - 1)
+            if n < GROUPS:
+                if n % SPINS == 0:
+                    sum_one_electron(n // SPINS)
+                sum_two_electron(n, 0)
+            if n > 0:
+                multiply_group(n - 1)
+            if n < GROUPS:
+                sum_two_electron(n, 1)
+                transpose_group(n)
+            if n > 0:
+                finish_group(n - 1)

@@ -23,6 +23,8 @@ PACK = 4
 BLOCKS = WALKERS // P
 GROUPS = BLOCKS * SPINS
 PAIRS = PER_SPIN // 2
+LOAD_AHEAD = 4
+QUARTER = P // PER_SPIN
 
 W_U, W_M_OWN, W_M_OTHER, W_E = 0, 1, 2, 3
 N_PASSES = 4
@@ -36,8 +38,9 @@ def tile_ferminetoneelectronlayer_pa_t_kernel(
     nc = tc.nc
     with ExitStack() as ctx:
         const = ctx.enter_context(tc.tile_pool(name="const", bufs=1))
-        x1_pool = ctx.enter_context(tc.tile_pool(name="x1", bufs=3))
+        x1_pool = ctx.enter_context(tc.tile_pool(name="x1", bufs=BLOCKS))
         e2_pool = ctx.enter_context(tc.tile_pool(name="e2", bufs=2 * PAIRS))
+        ty_pool = ctx.enter_context(tc.tile_pool(name="ty", bufs=2))
         work = ctx.enter_context(tc.tile_pool(name="work", bufs=2))
         out_pool = ctx.enter_context(tc.tile_pool(name="o", bufs=3))
         tp_pool = ctx.enter_context(tc.psum_pool(name="tp", bufs=4))
@@ -49,6 +52,12 @@ def tile_ferminetoneelectronlayer_pa_t_kernel(
         bias_bc = const.tile([P, D1], BF16)
         ident = const.tile([P, P], F32)
         make_identity(nc, ident[:])
+        fours = const.tile([P, QUARTER], F32)
+        nc.vector.tensor_reduce(
+            out=fours[:], in_=ident[:].rearrange("p (w j) -> p w j", j=PER_SPIN), axis=mybir.AxisListType.X, op=ADD
+        )
+        averager = const.tile([P, QUARTER], BF16)
+        nc.scalar.activation(out=averager[:], in_=fours[:], func=ACT.Copy, scale=1.0 / PER_SPIN)
 
         def load_weight(place, w_words, w_scales):
             last = place + w_words.shape[0]
@@ -61,40 +70,56 @@ def tile_ferminetoneelectronlayer_pa_t_kernel(
                     in_=w_scales[:, 4 * quad : 4 * quad + 4, :].rearrange("g r n -> r g n").bitcast(I32),
                 )
 
-        x1_of, e2_of, sums_of, grouped_of, codes_of, gb_of, o_of = {}, {}, {}, {}, {}, {}, {}
+        x1_of, e2_of, sums_of, grouped_of, codes_of, gb_of, acc_of, o_of = {}, {}, {}, {}, {}, {}, {}, {}
 
-        def load_group(n):
-            blk, spin = divmod(n, SPINS)
+        def block_and_spin(g):
+            return g // SPINS, 1 - g % SPINS
+
+        def load_group(g):
+            blk, spin = block_and_spin(g)
             walkers = slice(blk * P, (blk + 1) * P)
-            if spin == 0:
+            if spin == 1:
+                for pair in range(PAIRS):
+                    e2 = e2_pool.tile([P, 2, SPINS, PER_SPIN, D2], BF16)
+                    first = spin * PER_SPIN + 2 * pair
+                    for h in range(SPINS):
+                        partner = ((spin + h) % SPINS) * PER_SPIN
+                        nc.sync.dma_start(
+                            out=e2[:, :, h, :, :], in_=in_2e[walkers, first : first + 2, partner : partner + PER_SPIN, :]
+                        )
+                    e2_of[g, pair] = e2
+            else:
                 x1 = x1_pool.tile([P, SPINS * PER_SPIN, D1], BF16)
                 nc.sync.dma_start(out=x1[:], in_=in_1e[walkers])
                 x1_of[blk] = x1
-            for pair in range(PAIRS):
-                e2 = e2_pool.tile([P, 2, SPINS, PER_SPIN, D2], BF16)
-                first = spin * PER_SPIN + 2 * pair
-                for h in range(SPINS):
-                    partner = ((spin + h) % SPINS) * PER_SPIN
-                    nc.sync.dma_start(
-                        out=e2[:, :, h, :, :], in_=in_2e[walkers, first : first + 2, partner : partner + PER_SPIN, :]
-                    )
-                e2_of[n, pair] = e2
+                ty = ty_pool.tile([P, PER_SPIN, PER_SPIN, SPINS, D2], BF16)
+                for q in range(PER_SPIN):
+                    first_walker = blk * P + q * QUARTER
+                    for j in range(PER_SPIN):
+                        nc.sync.dma_start(
+                            out=ty[j:P:PER_SPIN, q],
+                            in_=in_2e[first_walker : first_walker + QUARTER, 0:PER_SPIN, j : SPINS * PER_SPIN : PER_SPIN, :],
+                        )
+                e2_of[g] = ty
 
-        def sum_one_electron(blk):
-            halves = x1_of[blk][:].rearrange("p (s h l) d -> p s h (l d)", s=SPINS, h=2, l=2)
-            m_half = work.tile([P, SPINS, 2 * D1], F32, bufs=1)
-            nc.vector.tensor_tensor(out=m_half[:], in0=halves[:, :, 0, :], in1=halves[:, :, 1, :], op=ADD)
-            m_sum = work.tile([P, SPINS, D1], BF16)
-            rest = m_half[:].rearrange("p s (l d) -> p s l d", l=2)
-            nc.vector.tensor_tensor(out=m_sum[:], in0=rest[:, :, 0, :], in1=rest[:, :, 1, :], op=ADD)
-            sums_of["m", blk] = m_sum
+        def sum_one_electron(blk, step):
+            if step == 0:
+                halves = x1_of[blk][:].rearrange("p (s h l) d -> p s h (l d)", s=SPINS, h=2, l=2)
+                m_half = work.tile([P, SPINS, 2 * D1], F32, bufs=1)
+                nc.vector.tensor_tensor(out=m_half[:], in0=halves[:, :, 0, :], in1=halves[:, :, 1, :], op=ADD)
+                sums_of["half", blk] = m_half
+            else:
+                m_sum = work.tile([P, SPINS, D1], BF16)
+                rest = sums_of["half", blk][:].rearrange("p s (l d) -> p s l d", l=2)
+                nc.vector.tensor_tensor(out=m_sum[:], in0=rest[:, :, 0, :], in1=rest[:, :, 1, :], op=ADD)
+                sums_of["m", blk] = m_sum
 
-        def sum_two_electron(n, pair):
+        def sum_two_electron(g, pair):
             if pair == 0:
                 a_sum = work.tile([P, PER_SPIN, SPINS * D2], BF16)
-                sums_of["a", n] = a_sum
-            a_sum = sums_of["a", n]
-            halves = e2_of[n, pair][:].rearrange("p i s (h l) d -> p (i s) h (l d)", h=2, l=2)
+                sums_of["a", g] = a_sum
+            a_sum = sums_of["a", g]
+            halves = e2_of[g, pair][:].rearrange("p i s (h l) d -> p (i s) h (l d)", h=2, l=2)
             a_half = work.tile([P, 2 * SPINS, 2 * D2], F32)
             nc.vector.tensor_tensor(out=a_half[:], in0=halves[:, :, 0, :], in1=halves[:, :, 1, :], op=ADD)
             rest = a_half[:].rearrange("p g (l d) -> p g l d", l=2)
@@ -128,24 +153,44 @@ def tile_ferminetoneelectronlayer_pa_t_kernel(
                         scale=1.0 / PER_SPIN,
                     )
 
-        def transpose_group(n):
-            blk, spin = divmod(n, SPINS)
+        def average_on_tensor(g, pair):
+            features = e2_of[g][:].rearrange("p q i s d -> p q i (s d)")
+            if pair == 0:
+                a_grouped = work.tile([P, PER_SPIN, P, PACK], BF16, align_bytes=64, bufs=3)
+                grouped_of["a", g] = a_grouped
+            grouped = grouped_of["a", g]
+            for i in range(2 * pair, 2 * pair + 2):
+                bank = tp_pool.tile([P, PACK, P], F32, tag="tp")
+                for t in range(PACK):
+                    for q in range(PER_SPIN):
+                        nc.tensor.matmul(
+                            out=bank[:, t, q * QUARTER : (q + 1) * QUARTER],
+                            lhsT=features[:, q, i, t : SPINS * D2 : PACK],
+                            rhs=averager[:],
+                            start=True,
+                            stop=True,
+                        )
+                nc.scalar.copy(out=grouped[:, i, :, :], in_=bank[:].rearrange("p t w -> p w t"))
+
+        def transpose_inputs(g):
+            blk, spin = block_and_spin(g)
             x_banks = transpose_rows(x1_of[blk][:, spin * PER_SPIN : (spin + 1) * PER_SPIN, :], PER_SPIN)
             x_grouped = work.tile([P, PER_SPIN, P, PACK], BF16, align_bytes=64)
             x_words = x_grouped[:].rearrange("p i w t -> p (i w t)").bitcast(F32)
             x_words = x_words.rearrange("p (i w u) -> p i w u", i=PER_SPIN, w=P, u=2)
             for b, bank in enumerate(x_banks):
                 nc.scalar.copy(out=x_words[:, 2 * b : 2 * b + 2], in_=bank[:].rearrange("p (r u) w -> p r w u", u=2))
-            grouped_of["x", n] = x_grouped
-            if spin == 0:
-                m_banks = transpose_rows(sums_of["m", blk][:], SPINS)
-                m_grouped = work.tile([P, SPINS, P, PACK], BF16, align_bytes=64)
-                copy_scaled(m_grouped, m_banks)
-                grouped_of["m", blk] = m_grouped
-            a_banks = transpose_rows(sums_of["a", n][:], PER_SPIN)
-            a_grouped = work.tile([P, PER_SPIN, P, PACK], BF16, align_bytes=64)
-            copy_scaled(a_grouped, a_banks)
-            grouped_of["a", n] = a_grouped
+            grouped_of["x", g] = x_grouped
+
+        def transpose_one_electron_sums(blk):
+            m_grouped = work.tile([P, SPINS, P, PACK], BF16, align_bytes=64)
+            copy_scaled(m_grouped, transpose_rows(sums_of["m", blk][:], SPINS))
+            grouped_of["m", blk] = m_grouped
+
+        def transpose_two_electron_sums(g):
+            a_grouped = work.tile([P, PER_SPIN, P, PACK], BF16, align_bytes=64, bufs=3)
+            copy_scaled(a_grouped, transpose_rows(sums_of["a", g][:], PER_SPIN))
+            grouped_of["a", g] = a_grouped
 
         def quantise(key, count):
             grouped = grouped_of[key]
@@ -158,12 +203,11 @@ def tile_ferminetoneelectronlayer_pa_t_kernel(
             )
             codes_of[key] = (codes, scales)
 
-        def quantise_group(n):
-            blk, spin = divmod(n, SPINS)
-            quantise(("x", n), PER_SPIN)
-            if spin == 0:
-                quantise(("m", blk), SPINS)
-            quantise(("a", n), PER_SPIN)
+        def quantise_group(g):
+            quantise(("x", g), PER_SPIN)
+            if g % SPINS == 0:
+                quantise(("m", g // SPINS), SPINS)
+            quantise(("a", g), PER_SPIN)
 
         def mx_pass(acc, key, row, place, start, stop):
             codes, scales = codes_of[key]
@@ -177,9 +221,9 @@ def tile_ferminetoneelectronlayer_pa_t_kernel(
                 stop=stop,
             )
 
-        def multiply_group(n):
-            blk, spin = divmod(n, SPINS)
-            if spin == 0:
+        def multiply_group(g):
+            if g % SPINS == 0:
+                blk = g // SPINS
                 gb = work.tile([P, SPINS, D1], F32)
                 for s in range(SPINS):
                     acc_g = acc_pool.tile([P, D1], F32, tag="acc")
@@ -187,40 +231,66 @@ def tile_ferminetoneelectronlayer_pa_t_kernel(
                     mx_pass(acc_g, ("m", blk), 1 - s, W_M_OTHER, False, True)
                     nc.vector.tensor_tensor(out=gb[:, s, :], in0=acc_g[:], in1=bias_bc[:], op=ADD)
                 gb_of[blk] = gb
-            o = out_pool.tile([P, PER_SPIN, D1], F32)
             for i in range(PER_SPIN):
                 acc = acc_pool.tile([P, D1], F32, tag="acc")
-                mx_pass(acc, ("x", n), i, W_U, True, False)
-                mx_pass(acc, ("a", n), i, W_E, False, True)
-                nc.vector.tensor_tensor(out=o[:, i, :], in0=acc[:], in1=gb_of[blk][:, spin, :], op=ADD)
-            nc.scalar.activation(out=o[:], in_=o[:], func=ACT.Tanh)
-            o_of[n] = o
+                mx_pass(acc, ("x", g), i, W_U, True, False)
+                mx_pass(acc, ("a", g), i, W_E, False, True)
+                acc_of[g, i] = acc
 
-        def finish_group(n):
-            blk, spin = divmod(n, SPINS)
-            electrons = slice(spin * PER_SPIN, (spin + 1) * PER_SPIN)
-            o = o_of[n]
-            nc.vector.tensor_tensor(out=o[:], in0=o[:], in1=x1_of[blk][:, electrons, :], op=ADD)
-            nc.sync.dma_start(out=out[blk * P : (blk + 1) * P, electrons, :], in_=o[:])
+        def leave_psum(g):
+            blk, spin = block_and_spin(g)
+            o = out_pool.tile([P, PER_SPIN, D1], F32)
+            for pair in range(PAIRS):
+                for i in range(2 * pair, 2 * pair + 2):
+                    nc.vector.tensor_tensor(out=o[:, i, :], in0=acc_of[g, i][:], in1=gb_of[blk][:, spin, :], op=ADD)
+                both = o[:, 2 * pair : 2 * pair + 2, :]
+                nc.scalar.activation(out=both, in_=both, func=ACT.Tanh)
+            o_of[g] = o
 
+        def finish_group(g):
+            blk, spin = block_and_spin(g)
+            for pair in range(PAIRS):
+                both = o_of[g][:, 2 * pair : 2 * pair + 2, :]
+                first = spin * PER_SPIN + 2 * pair
+                nc.vector.tensor_tensor(out=both, in0=both, in1=x1_of[blk][:, first : first + 2, :], op=ADD)
+                nc.sync.dma_start(out=out[blk * P : (blk + 1) * P, first : first + 2, :], in_=both)
+
+        def is_group(g):
+            return 0 <= g < GROUPS
+
+        ctx.enter_context(tc.manual_schedule())
         load_group(0)
+        load_group(1)
+        load_group(2)
         load_weight(W_U, wu_words, wu_scales)
         load_weight(W_M_OWN, wm_words, wm_scales)
         load_weight(W_E, w2_words, w2_scales)
         nc.sync.dma_start(out=bias_bc[:], in_=b_unmixed.partition_broadcast(P))
-        for n in range(GROUPS + 1):
-            if n + 1 < GROUPS:
-                load_group(n + 1)
-            if n > 0:
+        load_group(3)
+        for n in range(-2, GROUPS + 3):
+            odd = n % 2
+            if n >= 0 and is_group(n + LOAD_AHEAD):
+                load_group(n + LOAD_AHEAD)
+            if is_group(n):
+                transpose_inputs(n)
+            if odd:
+                if is_group(n + 1):
+                    sum_two_electron(n + 1, 1)
+                    transpose_two_electron_sums(n + 1)
+                    sum_one_electron((n + 1) // SPINS, 0)
+            else:
+                if is_group(n):
+                    sum_one_electron(n // SPINS, 1)
+                    transpose_one_electron_sums(n // SPINS)
+                if is_group(n + 2):
+                    sum_two_electron(n + 2, 0)
+            if is_group(n - 3):
+                finish_group(n - 3)
+            if is_group(n - 1):
                 quantise_group(n - 1)
-            if n < GROUPS:
-                if n % SPINS == 0:
-                    sum_one_electron(n // SPINS)
-                sum_two_electron(n, 0)
-            if n > 0:
+            if is_group(n - 2):
+                leave_psum(n - 2)
+            if is_group(n - 1):
                 multiply_group(n - 1)
-            if n < GROUPS:
-                sum_two_electron(n, 1)
-                transpose_group(n)
-            if n > 0:
-                finish_group(n - 1)
+            if is_group(n + 1 + odd):
+                average_on_tensor(n + 1 + odd, 1 - odd)

@@ -27,7 +27,8 @@ LOAD_AHEAD = 4
 QUARTER = P // PER_SPIN
 
 W_U, W_M_OWN, W_M_OTHER, W_E = 0, 1, 2, 3
-N_PASSES = 4
+N_PASSES = 5
+HALF = P // 2
 
 FLOPS = 2 * WALKERS * 8 * D1 * D1 * 2 + 2 * WALKERS * SPINS * (SPINS * D1) * D1
 
@@ -39,8 +40,7 @@ def tile_ferminetoneelectronlayer_pa_t_kernel(
     with ExitStack() as ctx:
         const = ctx.enter_context(tc.tile_pool(name="const", bufs=1))
         x1_pool = ctx.enter_context(tc.tile_pool(name="x1", bufs=BLOCKS))
-        e2_pool = ctx.enter_context(tc.tile_pool(name="e2", bufs=2 * PAIRS))
-        ty_pool = ctx.enter_context(tc.tile_pool(name="ty", bufs=2))
+        ty_pool = ctx.enter_context(tc.tile_pool(name="ty", bufs=LOAD_AHEAD + 2))
         work = ctx.enter_context(tc.tile_pool(name="work", bufs=2))
         out_pool = ctx.enter_context(tc.tile_pool(name="o", bufs=3))
         tp_pool = ctx.enter_context(tc.psum_pool(name="tp", bufs=4))
@@ -70,65 +70,60 @@ def tile_ferminetoneelectronlayer_pa_t_kernel(
                     in_=w_scales[:, 4 * quad : 4 * quad + 4, :].rearrange("g r n -> r g n").bitcast(I32),
                 )
 
+        def load_exchanged_weight(place, w_words, w_scales):
+            for h in range(2):
+                nc.sync.dma_start(
+                    out=words[h * HALF : (h + 1) * HALF, place, :].bitcast(I32),
+                    in_=w_words[0, (1 - h) * HALF : (2 - h) * HALF, :].bitcast(I32),
+                )
+            for quad in range(4):
+                row = 4 * ((quad + 2) % 4)
+                nc.sync.dma_start(
+                    out=planes[32 * quad : 32 * quad + 4, place, :].bitcast(I32),
+                    in_=w_scales[0, row : row + 4, :].bitcast(I32),
+                )
+
         x1_of, e2_of, sums_of, grouped_of, codes_of, gb_of, acc_of, o_of = {}, {}, {}, {}, {}, {}, {}, {}
 
         def block_and_spin(g):
-            return g // SPINS, 1 - g % SPINS
+            return g // SPINS, g % SPINS
+
+        def load_one_electron(blk):
+            x1 = x1_pool.tile([P, SPINS * PER_SPIN, D1], BF16)
+            nc.sync.dma_start(out=x1[:], in_=in_1e[blk * P : (blk + 1) * P])
+            x1_of[blk] = x1
+
+        def load_two_electron(g):
+            blk, spin = block_and_spin(g)
+            ty = ty_pool.tile([P, PER_SPIN, PER_SPIN, SPINS, D2], BF16)
+            first = spin * PER_SPIN
+            for q in range(PER_SPIN):
+                first_walker = blk * P + q * QUARTER
+                for j in range(PER_SPIN):
+                    nc.sync.dma_start(
+                        out=ty[j:P:PER_SPIN, q],
+                        in_=in_2e[
+                            first_walker : first_walker + QUARTER,
+                            first : first + PER_SPIN,
+                            j : SPINS * PER_SPIN : PER_SPIN,
+                            :,
+                        ],
+                    )
+            e2_of[g] = ty
 
         def load_group(g):
-            blk, spin = block_and_spin(g)
-            walkers = slice(blk * P, (blk + 1) * P)
-            if spin == 1:
-                for pair in range(PAIRS):
-                    e2 = e2_pool.tile([P, 2, SPINS, PER_SPIN, D2], BF16)
-                    first = spin * PER_SPIN + 2 * pair
-                    for h in range(SPINS):
-                        partner = ((spin + h) % SPINS) * PER_SPIN
-                        nc.sync.dma_start(
-                            out=e2[:, :, h, :, :], in_=in_2e[walkers, first : first + 2, partner : partner + PER_SPIN, :]
-                        )
-                    e2_of[g, pair] = e2
-            else:
-                x1 = x1_pool.tile([P, SPINS * PER_SPIN, D1], BF16)
-                nc.sync.dma_start(out=x1[:], in_=in_1e[walkers])
-                x1_of[blk] = x1
-                ty = ty_pool.tile([P, PER_SPIN, PER_SPIN, SPINS, D2], BF16)
-                for q in range(PER_SPIN):
-                    first_walker = blk * P + q * QUARTER
-                    for j in range(PER_SPIN):
-                        nc.sync.dma_start(
-                            out=ty[j:P:PER_SPIN, q],
-                            in_=in_2e[first_walker : first_walker + QUARTER, 0:PER_SPIN, j : SPINS * PER_SPIN : PER_SPIN, :],
-                        )
-                e2_of[g] = ty
+            if g % SPINS == 0:
+                load_one_electron(g // SPINS)
+            load_two_electron(g)
 
-        def sum_one_electron(blk, step):
-            if step == 0:
-                halves = x1_of[blk][:].rearrange("p (s h l) d -> p s h (l d)", s=SPINS, h=2, l=2)
-                m_half = work.tile([P, SPINS, 2 * D1], F32, bufs=1)
-                nc.vector.tensor_tensor(out=m_half[:], in0=halves[:, :, 0, :], in1=halves[:, :, 1, :], op=ADD)
-                sums_of["half", blk] = m_half
-            else:
-                m_sum = work.tile([P, SPINS, D1], BF16)
-                rest = sums_of["half", blk][:].rearrange("p s (l d) -> p s l d", l=2)
-                nc.vector.tensor_tensor(out=m_sum[:], in0=rest[:, :, 0, :], in1=rest[:, :, 1, :], op=ADD)
-                sums_of["m", blk] = m_sum
-
-        def sum_two_electron(g, pair):
-            if pair == 0:
-                a_sum = work.tile([P, PER_SPIN, SPINS * D2], BF16)
-                sums_of["a", g] = a_sum
-            a_sum = sums_of["a", g]
-            halves = e2_of[g, pair][:].rearrange("p i s (h l) d -> p (i s) h (l d)", h=2, l=2)
-            a_half = work.tile([P, 2 * SPINS, 2 * D2], F32)
-            nc.vector.tensor_tensor(out=a_half[:], in0=halves[:, :, 0, :], in1=halves[:, :, 1, :], op=ADD)
-            rest = a_half[:].rearrange("p g (l d) -> p g l d", l=2)
-            nc.vector.tensor_tensor(
-                out=a_sum[:, 2 * pair : 2 * pair + 2, :].rearrange("p i (s d) -> p (i s) d", s=SPINS),
-                in0=rest[:, :, 0, :],
-                in1=rest[:, :, 1, :],
-                op=ADD,
-            )
+        def sum_one_electron(blk):
+            halves = x1_of[blk][:].rearrange("p (s h l) d -> p s h (l d)", s=SPINS, h=2, l=2)
+            m_half = work.tile([P, SPINS, 2 * D1], F32, bufs=1)
+            nc.vector.tensor_tensor(out=m_half[:], in0=halves[:, :, 0, :], in1=halves[:, :, 1, :], op=ADD)
+            m_sum = work.tile([P, SPINS, D1], BF16)
+            rest = m_half[:].rearrange("p s (l d) -> p s l d", l=2)
+            nc.vector.tensor_tensor(out=m_sum[:], in0=rest[:, :, 0, :], in1=rest[:, :, 1, :], op=ADD)
+            sums_of["m", blk] = m_sum
 
         def transpose_rows(rows, count):
             as_words = rows.bitcast(F32)
@@ -153,24 +148,25 @@ def tile_ferminetoneelectronlayer_pa_t_kernel(
                         scale=1.0 / PER_SPIN,
                     )
 
-        def average_on_tensor(g, pair):
+        def average_two_electron(g):
             features = e2_of[g][:].rearrange("p q i s d -> p q i (s d)")
-            if pair == 0:
-                a_grouped = work.tile([P, PER_SPIN, P, PACK], BF16, align_bytes=64, bufs=3)
-                grouped_of["a", g] = a_grouped
-            grouped = grouped_of["a", g]
-            for i in range(2 * pair, 2 * pair + 2):
-                bank = tp_pool.tile([P, PACK, P], F32, tag="tp")
-                for t in range(PACK):
-                    for q in range(PER_SPIN):
-                        nc.tensor.matmul(
-                            out=bank[:, t, q * QUARTER : (q + 1) * QUARTER],
-                            lhsT=features[:, q, i, t : SPINS * D2 : PACK],
-                            rhs=averager[:],
-                            start=True,
-                            stop=True,
-                        )
-                nc.scalar.copy(out=grouped[:, i, :, :], in_=bank[:].rearrange("p t w -> p w t"))
+            grouped = work.tile([P, PER_SPIN, P, PACK], BF16, align_bytes=64, bufs=3, name="a_grouped")
+            for pair in range(PAIRS):
+                bank = tp_pool.tile([P, 2, PACK, P], BF16, tag="tp")
+                for q in range(PER_SPIN):
+                    for e in range(2):
+                        for t in range(PACK):
+                            nc.tensor.matmul(
+                                out=bank[:, e, t, q * QUARTER : (q + 1) * QUARTER],
+                                lhsT=features[:, q, 2 * pair + e, t : SPINS * D2 : PACK],
+                                rhs=averager[:],
+                                start=True,
+                                stop=True,
+                            )
+                nc.scalar.copy(
+                    out=grouped[:, 2 * pair : 2 * pair + 2, :, :], in_=bank[:].rearrange("p e t w -> p e w t")
+                )
+            grouped_of["a", g] = grouped
 
         def transpose_inputs(g):
             blk, spin = block_and_spin(g)
@@ -186,11 +182,6 @@ def tile_ferminetoneelectronlayer_pa_t_kernel(
             m_grouped = work.tile([P, SPINS, P, PACK], BF16, align_bytes=64)
             copy_scaled(m_grouped, transpose_rows(sums_of["m", blk][:], SPINS))
             grouped_of["m", blk] = m_grouped
-
-        def transpose_two_electron_sums(g):
-            a_grouped = work.tile([P, PER_SPIN, P, PACK], BF16, align_bytes=64, bufs=3)
-            copy_scaled(a_grouped, transpose_rows(sums_of["a", g][:], PER_SPIN))
-            grouped_of["a", g] = a_grouped
 
         def quantise(key, count):
             grouped = grouped_of[key]
@@ -234,7 +225,7 @@ def tile_ferminetoneelectronlayer_pa_t_kernel(
             for i in range(PER_SPIN):
                 acc = acc_pool.tile([P, D1], F32, tag="acc")
                 mx_pass(acc, ("x", g), i, W_U, True, False)
-                mx_pass(acc, ("a", g), i, W_E, False, True)
+                mx_pass(acc, ("a", g), i, W_E + g % SPINS, False, True)
                 acc_of[g, i] = acc
 
         def leave_psum(g):
@@ -260,37 +251,29 @@ def tile_ferminetoneelectronlayer_pa_t_kernel(
 
         ctx.enter_context(tc.manual_schedule())
         load_group(0)
-        load_group(1)
-        load_group(2)
         load_weight(W_U, wu_words, wu_scales)
         load_weight(W_M_OWN, wm_words, wm_scales)
         load_weight(W_E, w2_words, w2_scales)
+        load_exchanged_weight(W_E + 1, w2_words, w2_scales)
         nc.sync.dma_start(out=bias_bc[:], in_=b_unmixed.partition_broadcast(P))
-        load_group(3)
-        for n in range(-2, GROUPS + 3):
-            odd = n % 2
+        for g in range(1, LOAD_AHEAD):
+            load_group(g)
+        for n in range(-1, GROUPS + 3):
             if n >= 0 and is_group(n + LOAD_AHEAD):
                 load_group(n + LOAD_AHEAD)
             if is_group(n):
                 transpose_inputs(n)
-            if odd:
-                if is_group(n + 1):
-                    sum_two_electron(n + 1, 1)
-                    transpose_two_electron_sums(n + 1)
-                    sum_one_electron((n + 1) // SPINS, 0)
-            else:
-                if is_group(n):
-                    sum_one_electron(n // SPINS, 1)
+                if n % SPINS == 0:
                     transpose_one_electron_sums(n // SPINS)
-                if is_group(n + 2):
-                    sum_two_electron(n + 2, 0)
-            if is_group(n - 3):
-                finish_group(n - 3)
             if is_group(n - 1):
                 quantise_group(n - 1)
             if is_group(n - 2):
                 leave_psum(n - 2)
             if is_group(n - 1):
                 multiply_group(n - 1)
-            if is_group(n + 1 + odd):
-                average_on_tensor(n + 1 + odd, 1 - odd)
+            if is_group(n - 3):
+                finish_group(n - 3)
+            if is_group(n + 1):
+                if (n + 1) % SPINS == 0:
+                    sum_one_electron((n + 1) // SPINS)
+                average_two_electron(n + 1)

@@ -22,8 +22,11 @@ D2 = 256
 PACK = 4
 BLOCKS = WALKERS // P
 GROUPS = BLOCKS * SPINS
-PAIRS = PER_SPIN // 2
-LOAD_AHEAD = 4
+PAIR = 2
+UNITS_PER_GROUP = PER_SPIN // PAIR
+UNITS_PER_BLOCK = UNITS_PER_GROUP * SPINS
+UNITS = GROUPS * UNITS_PER_GROUP
+GROUPS_AHEAD = 6
 QUARTER = P // PER_SPIN
 
 W_U, W_M_OWN, W_M_OTHER, W_E = 0, 1, 2, 3
@@ -40,11 +43,13 @@ def tile_ferminetoneelectronlayer_pa_t_kernel(
     with ExitStack() as ctx:
         const = ctx.enter_context(tc.tile_pool(name="const", bufs=1))
         x1_pool = ctx.enter_context(tc.tile_pool(name="x1", bufs=BLOCKS))
-        ty_pool = ctx.enter_context(tc.tile_pool(name="ty", bufs=LOAD_AHEAD + 2))
+        ty_pool = ctx.enter_context(tc.tile_pool(name="ty", bufs=GROUPS_AHEAD))
         work = ctx.enter_context(tc.tile_pool(name="work", bufs=2))
-        out_pool = ctx.enter_context(tc.tile_pool(name="o", bufs=3))
+        out_pool = ctx.enter_context(tc.tile_pool(name="o", bufs=4))
         tp_pool = ctx.enter_context(tc.psum_pool(name="tp", bufs=4))
         acc_pool = ctx.enter_context(tc.psum_pool(name="acc", bufs=4))
+
+        ctx.enter_context(tc.manual_schedule())
 
         planes = const.tile([P, N_PASSES, D1], U8, align_bytes=64)
         nc.vector.memset(planes[:].rearrange("p w n -> p (w n)").bitcast(I32), 0)
@@ -83,10 +88,10 @@ def tile_ferminetoneelectronlayer_pa_t_kernel(
                     in_=w_scales[0, row : row + 4, :].bitcast(I32),
                 )
 
-        x1_of, e2_of, sums_of, grouped_of, codes_of, gb_of, acc_of, o_of = {}, {}, {}, {}, {}, {}, {}, {}
+        def block_and_electron(unit):
+            return unit // UNITS_PER_BLOCK, PAIR * (unit % UNITS_PER_BLOCK)
 
-        def block_and_spin(g):
-            return g // SPINS, g % SPINS
+        x1_of, e2_of, sums_of, grouped_of, codes_of, gb_of, acc_of, o_of = {}, {}, {}, {}, {}, {}, {}, {}
 
         def load_one_electron(blk):
             x1 = x1_pool.tile([P, SPINS * PER_SPIN, D1], BF16)
@@ -94,9 +99,8 @@ def tile_ferminetoneelectronlayer_pa_t_kernel(
             x1_of[blk] = x1
 
         def load_two_electron(g):
-            blk, spin = block_and_spin(g)
+            blk, electron = block_and_electron(UNITS_PER_GROUP * g)
             ty = ty_pool.tile([P, PER_SPIN, PER_SPIN, SPINS, D2], BF16)
-            first = spin * PER_SPIN
             for q in range(PER_SPIN):
                 first_walker = blk * P + q * QUARTER
                 for j in range(PER_SPIN):
@@ -104,7 +108,7 @@ def tile_ferminetoneelectronlayer_pa_t_kernel(
                         out=ty[j:P:PER_SPIN, q],
                         in_=in_2e[
                             first_walker : first_walker + QUARTER,
-                            first : first + PER_SPIN,
+                            electron : electron + PER_SPIN,
                             j : SPINS * PER_SPIN : PER_SPIN,
                             :,
                         ],
@@ -116,77 +120,71 @@ def tile_ferminetoneelectronlayer_pa_t_kernel(
                 load_one_electron(g // SPINS)
             load_two_electron(g)
 
-        def sum_one_electron(blk):
-            halves = x1_of[blk][:].rearrange("p (s h l) d -> p s h (l d)", s=SPINS, h=2, l=2)
-            m_half = work.tile([P, SPINS, 2 * D1], F32, bufs=1)
-            nc.vector.tensor_tensor(out=m_half[:], in0=halves[:, :, 0, :], in1=halves[:, :, 1, :], op=ADD)
-            m_sum = work.tile([P, SPINS, D1], BF16)
-            rest = m_half[:].rearrange("p s (l d) -> p s l d", l=2)
-            nc.vector.tensor_tensor(out=m_sum[:], in0=rest[:, :, 0, :], in1=rest[:, :, 1, :], op=ADD)
-            sums_of["m", blk] = m_sum
+        def sum_one_electron(blk, step):
+            if step == 0:
+                halves = x1_of[blk][:].rearrange("p (s h l) d -> p s h (l d)", s=SPINS, h=2, l=2)
+                m_half = work.tile([P, SPINS, 2 * D1], F32, bufs=1)
+                nc.vector.tensor_tensor(out=m_half[:], in0=halves[:, :, 0, :], in1=halves[:, :, 1, :], op=ADD)
+                sums_of["half", blk] = m_half
+            else:
+                m_sum = work.tile([P, SPINS, D1], BF16)
+                rest = sums_of["half", blk][:].rearrange("p s (l d) -> p s l d", l=2)
+                nc.vector.tensor_tensor(out=m_sum[:], in0=rest[:, :, 0, :], in1=rest[:, :, 1, :], op=ADD)
+                sums_of["m", blk] = m_sum
 
-        def transpose_rows(rows, count):
+        def transpose_rows(rows):
             as_words = rows.bitcast(F32)
-            banks = []
-            for first in range(0, count, 2):
-                bank = tp_pool.tile([P, 2 * 2, P], F32, tag="tp")
-                for r in range(2):
-                    for u in range(2):
-                        nc.tensor.transpose(bank[:, 2 * r + u, :], as_words[:, first + r, u : D1 // 2 : 2], ident[:])
-                banks.append(bank)
-            return banks
+            bank = tp_pool.tile([P, 2 * 2, P], F32, tag="tp")
+            for r in range(2):
+                for u in range(2):
+                    nc.tensor.transpose(bank[:, 2 * r + u, :], as_words[:, r, u : D1 // 2 : 2], ident[:])
+            return bank
 
-        def copy_scaled(grouped, banks):
-            for b, bank in enumerate(banks):
-                values = bank[:].rearrange("p a w -> p (a w)").bitcast(BF16)
-                values = values.rearrange("p (r u w e) -> p r w u e", r=2, u=2, w=P, e=2)
-                for r in range(2):
-                    nc.scalar.activation(
-                        out=grouped[:, 2 * b + r, :, :].rearrange("p w (u e) -> p w u e", u=2),
-                        in_=values[:, r],
-                        func=ACT.Copy,
-                        scale=1.0 / PER_SPIN,
-                    )
+        def average_two_electron(unit):
+            first = PAIR * (unit % UNITS_PER_GROUP)
+            features = e2_of[unit // UNITS_PER_GROUP][:].rearrange("p q i s d -> p q i (s d)")
+            a_grouped = work.tile([P, PAIR, P, PACK], BF16, align_bytes=64, bufs=3)
+            bank = tp_pool.tile([P, PAIR, PACK, P], BF16, tag="tp")
+            for q in range(PER_SPIN):
+                for e in range(PAIR):
+                    for t in range(PACK):
+                        nc.tensor.matmul(
+                            out=bank[:, e, t, q * QUARTER : (q + 1) * QUARTER],
+                            lhsT=features[:, q, first + e, t : SPINS * D2 : PACK],
+                            rhs=averager[:],
+                            start=True,
+                            stop=True,
+                        )
+            nc.scalar.copy(out=a_grouped[:], in_=bank[:].rearrange("p e t w -> p e w t"))
+            grouped_of["a", unit] = a_grouped
 
-        def average_two_electron(g):
-            features = e2_of[g][:].rearrange("p q i s d -> p q i (s d)")
-            grouped = work.tile([P, PER_SPIN, P, PACK], BF16, align_bytes=64, bufs=3, name="a_grouped")
-            for pair in range(PAIRS):
-                bank = tp_pool.tile([P, 2, PACK, P], BF16, tag="tp")
-                for q in range(PER_SPIN):
-                    for e in range(2):
-                        for t in range(PACK):
-                            nc.tensor.matmul(
-                                out=bank[:, e, t, q * QUARTER : (q + 1) * QUARTER],
-                                lhsT=features[:, q, 2 * pair + e, t : SPINS * D2 : PACK],
-                                rhs=averager[:],
-                                start=True,
-                                stop=True,
-                            )
-                nc.scalar.copy(
-                    out=grouped[:, 2 * pair : 2 * pair + 2, :, :], in_=bank[:].rearrange("p e t w -> p e w t")
-                )
-            grouped_of["a", g] = grouped
-
-        def transpose_inputs(g):
-            blk, spin = block_and_spin(g)
-            x_banks = transpose_rows(x1_of[blk][:, spin * PER_SPIN : (spin + 1) * PER_SPIN, :], PER_SPIN)
-            x_grouped = work.tile([P, PER_SPIN, P, PACK], BF16, align_bytes=64)
+        def transpose_inputs(unit):
+            blk, electron = block_and_electron(unit)
+            bank = transpose_rows(x1_of[blk][:, electron : electron + PAIR, :])
+            x_grouped = work.tile([P, PAIR, P, PACK], BF16, align_bytes=64)
             x_words = x_grouped[:].rearrange("p i w t -> p (i w t)").bitcast(F32)
-            x_words = x_words.rearrange("p (i w u) -> p i w u", i=PER_SPIN, w=P, u=2)
-            for b, bank in enumerate(x_banks):
-                nc.scalar.copy(out=x_words[:, 2 * b : 2 * b + 2], in_=bank[:].rearrange("p (r u) w -> p r w u", u=2))
-            grouped_of["x", g] = x_grouped
+            x_words = x_words.rearrange("p (i w u) -> p i w u", i=PAIR, w=P, u=2)
+            nc.scalar.copy(out=x_words, in_=bank[:].rearrange("p (r u) w -> p r w u", u=2))
+            grouped_of["x", unit] = x_grouped
 
         def transpose_one_electron_sums(blk):
+            bank = transpose_rows(sums_of["m", blk][:])
             m_grouped = work.tile([P, SPINS, P, PACK], BF16, align_bytes=64)
-            copy_scaled(m_grouped, transpose_rows(sums_of["m", blk][:], SPINS))
+            values = bank[:].rearrange("p a w -> p (a w)").bitcast(BF16)
+            values = values.rearrange("p (r u w e) -> p r w u e", r=2, u=2, w=P, e=2)
+            for s in range(SPINS):
+                nc.scalar.activation(
+                    out=m_grouped[:, s, :, :].rearrange("p w (u e) -> p w u e", u=2),
+                    in_=values[:, s],
+                    func=ACT.Copy,
+                    scale=1.0 / PER_SPIN,
+                )
             grouped_of["m", blk] = m_grouped
 
-        def quantise(key, count):
+        def quantise(key):
             grouped = grouped_of[key]
-            codes = work.tile([P, count, P], U32, align_bytes=64, tag="codes_" + key[0])
-            scales = work.tile([P, count, P], U8, align_bytes=64, tag="scales_" + key[0])
+            codes = work.tile([P, 2, P], U32, align_bytes=64, tag="codes_" + key[0])
+            scales = work.tile([P, 2, P], U8, align_bytes=64, tag="scales_" + key[0])
             nc.vector.quantize_mx(
                 out=codes[:].rearrange("p i w -> p (i w)").bitcast(FP8X4),
                 scales=scales[:].rearrange("p i w -> p (i w)"),
@@ -194,11 +192,11 @@ def tile_ferminetoneelectronlayer_pa_t_kernel(
             )
             codes_of[key] = (codes, scales)
 
-        def quantise_group(g):
-            quantise(("x", g), PER_SPIN)
-            if g % SPINS == 0:
-                quantise(("m", g // SPINS), SPINS)
-            quantise(("a", g), PER_SPIN)
+        def quantise_unit(unit):
+            if unit % UNITS_PER_BLOCK == 0:
+                quantise(("m", unit // UNITS_PER_BLOCK))
+            quantise(("x", unit))
+            quantise(("a", unit))
 
         def mx_pass(acc, key, row, place, start, stop):
             codes, scales = codes_of[key]
@@ -212,9 +210,9 @@ def tile_ferminetoneelectronlayer_pa_t_kernel(
                 stop=stop,
             )
 
-        def multiply_group(g):
-            if g % SPINS == 0:
-                blk = g // SPINS
+        def multiply_unit(unit):
+            blk, electron = block_and_electron(unit)
+            if unit % UNITS_PER_BLOCK == 0:
                 gb = work.tile([P, SPINS, D1], F32)
                 for s in range(SPINS):
                     acc_g = acc_pool.tile([P, D1], F32, tag="acc")
@@ -222,58 +220,58 @@ def tile_ferminetoneelectronlayer_pa_t_kernel(
                     mx_pass(acc_g, ("m", blk), 1 - s, W_M_OTHER, False, True)
                     nc.vector.tensor_tensor(out=gb[:, s, :], in0=acc_g[:], in1=bias_bc[:], op=ADD)
                 gb_of[blk] = gb
-            for i in range(PER_SPIN):
+            for i in range(PAIR):
                 acc = acc_pool.tile([P, D1], F32, tag="acc")
-                mx_pass(acc, ("x", g), i, W_U, True, False)
-                mx_pass(acc, ("a", g), i, W_E + g % SPINS, False, True)
-                acc_of[g, i] = acc
+                mx_pass(acc, ("x", unit), i, W_U, True, False)
+                mx_pass(acc, ("a", unit), i, W_E + electron // PER_SPIN, False, True)
+                acc_of[unit, i] = acc
 
-        def leave_psum(g):
-            blk, spin = block_and_spin(g)
-            o = out_pool.tile([P, PER_SPIN, D1], F32)
-            for pair in range(PAIRS):
-                for i in range(2 * pair, 2 * pair + 2):
-                    nc.vector.tensor_tensor(out=o[:, i, :], in0=acc_of[g, i][:], in1=gb_of[blk][:, spin, :], op=ADD)
-                both = o[:, 2 * pair : 2 * pair + 2, :]
-                nc.scalar.activation(out=both, in_=both, func=ACT.Tanh)
-            o_of[g] = o
+        def leave_psum(unit):
+            blk, electron = block_and_electron(unit)
+            o = out_pool.tile([P, PAIR, D1], F32)
+            for i in range(PAIR):
+                nc.vector.tensor_tensor(
+                    out=o[:, i, :], in0=acc_of[unit, i][:], in1=gb_of[blk][:, electron // PER_SPIN, :], op=ADD
+                )
+            nc.scalar.activation(out=o[:], in_=o[:], func=ACT.Tanh)
+            o_of[unit] = o
 
-        def finish_group(g):
-            blk, spin = block_and_spin(g)
-            for pair in range(PAIRS):
-                both = o_of[g][:, 2 * pair : 2 * pair + 2, :]
-                first = spin * PER_SPIN + 2 * pair
-                nc.vector.tensor_tensor(out=both, in0=both, in1=x1_of[blk][:, first : first + 2, :], op=ADD)
-                nc.sync.dma_start(out=out[blk * P : (blk + 1) * P, first : first + 2, :], in_=both)
+        def finish_unit(unit):
+            blk, electron = block_and_electron(unit)
+            o = o_of[unit]
+            nc.vector.tensor_tensor(out=o[:], in0=o[:], in1=x1_of[blk][:, electron : electron + PAIR, :], op=ADD)
+            nc.gpsimd.dma_start(out=out[blk * P : (blk + 1) * P, electron : electron + PAIR, :], in_=o[:])
 
-        def is_group(g):
-            return 0 <= g < GROUPS
+        def is_unit(unit):
+            return 0 <= unit < UNITS
 
-        ctx.enter_context(tc.manual_schedule())
         load_group(0)
-        load_weight(W_U, wu_words, wu_scales)
         load_weight(W_M_OWN, wm_words, wm_scales)
+        load_weight(W_U, wu_words, wu_scales)
         load_weight(W_E, w2_words, w2_scales)
-        load_exchanged_weight(W_E + 1, w2_words, w2_scales)
         nc.sync.dma_start(out=bias_bc[:], in_=b_unmixed.partition_broadcast(P))
-        for g in range(1, LOAD_AHEAD):
+        load_group(1)
+        load_exchanged_weight(W_E + 1, w2_words, w2_scales)
+        for g in range(2, GROUPS_AHEAD):
             load_group(g)
-        for n in range(-1, GROUPS + 3):
-            if n >= 0 and is_group(n + LOAD_AHEAD):
-                load_group(n + LOAD_AHEAD)
-            if is_group(n):
+        for n in range(-2, UNITS + 3):
+            if is_unit(n):
                 transpose_inputs(n)
-                if n % SPINS == 0:
-                    transpose_one_electron_sums(n // SPINS)
-            if is_group(n - 1):
-                quantise_group(n - 1)
-            if is_group(n - 2):
+                if n % UNITS_PER_BLOCK == 0:
+                    transpose_one_electron_sums(n // UNITS_PER_BLOCK)
+            if is_unit(n - 1):
+                quantise_unit(n - 1)
+            if is_unit(n - 2):
                 leave_psum(n - 2)
-            if is_group(n - 1):
-                multiply_group(n - 1)
-            if is_group(n - 3):
-                finish_group(n - 3)
-            if is_group(n + 1):
-                if (n + 1) % SPINS == 0:
-                    sum_one_electron((n + 1) // SPINS)
+            if is_unit(n - 1):
+                multiply_unit(n - 1)
+            if is_unit(n - 3):
+                finish_unit(n - 3)
+            for step in range(2):
+                if is_unit(n + 2 - step) and (n + 2 - step) % UNITS_PER_BLOCK == 0:
+                    sum_one_electron((n + 2 - step) // UNITS_PER_BLOCK, step)
+            if is_unit(n + 1):
                 average_two_electron(n + 1)
+            ahead = n // UNITS_PER_GROUP + GROUPS_AHEAD
+            if n >= 0 and n % UNITS_PER_GROUP == 0 and ahead < GROUPS:
+                load_group(ahead)

@@ -26,6 +26,7 @@ PAIR = 2
 UNITS_PER_GROUP = PER_SPIN // PAIR
 UNITS_PER_BLOCK = UNITS_PER_GROUP * SPINS
 UNITS = GROUPS * UNITS_PER_GROUP
+OUT_TILES = 12
 GROUPS_AHEAD = 6
 QUARTER = P // PER_SPIN
 
@@ -45,7 +46,7 @@ def tile_ferminetoneelectronlayer_pa_t_kernel(
         x1_pool = ctx.enter_context(tc.tile_pool(name="x1", bufs=BLOCKS))
         ty_pool = ctx.enter_context(tc.tile_pool(name="ty", bufs=GROUPS_AHEAD))
         work = ctx.enter_context(tc.tile_pool(name="work", bufs=2))
-        out_pool = ctx.enter_context(tc.tile_pool(name="o", bufs=4))
+        out_pool = ctx.enter_context(tc.tile_pool(name="o", bufs=OUT_TILES))
         tp_pool = ctx.enter_context(tc.psum_pool(name="tp", bufs=4))
         acc_pool = ctx.enter_context(tc.psum_pool(name="acc", bufs=4))
 
@@ -240,7 +241,7 @@ def tile_ferminetoneelectronlayer_pa_t_kernel(
             blk, electron = block_and_electron(unit)
             o = o_of[unit]
             nc.vector.tensor_tensor(out=o[:], in0=o[:], in1=x1_of[blk][:, electron : electron + PAIR, :], op=ADD)
-            nc.gpsimd.dma_start(out=out[blk * P : (blk + 1) * P, electron : electron + PAIR, :], in_=o[:])
+            nc.sync.dma_start(out=out[blk * P : (blk + 1) * P, electron : electron + PAIR, :], in_=o[:])
 
         def is_unit(unit):
             return 0 <= unit < UNITS

@@ -64,30 +64,35 @@ def tile_ferminetoneelectronlayer_pa_t_kernel(
         )
         averager = const.tile([P, QUARTER], BF16)
         nc.scalar.activation(out=averager[:], in_=fours[:], func=ACT.Copy, scale=1.0 / PER_SPIN)
+        ident_bf16 = const.tile([P, P], BF16)
+        nc.vector.tensor_copy(out=ident_bf16[:], in_=ident[:])
+        bias_col = const.tile([P, PACK], BF16)
+        nc.gpsimd.dma_start(out=bias_col[:], in_=b_unmixed.rearrange("(p t) -> p t", t=PACK))
+        bias_bank = tp_pool.tile([P, PACK, P], BF16, tag="tp")
+        for t in range(PACK):
+            nc.tensor.transpose(bias_bank[:, t, :], bias_col[:, t : t + 1].to_broadcast([P, P]), ident_bf16[:])
+        nc.scalar.copy(
+            out=bias_bc[:].rearrange("p (k t) -> p k t", t=PACK), in_=bias_bank[:].rearrange("p t k -> p k t")
+        )
 
-        def load_weight(place, w_words, w_scales):
+        def weight_loads(place, w_words, w_scales):
             last = place + w_words.shape[0]
-            nc.sync.dma_start(
-                out=words[:, place:last, :].bitcast(I32), in_=w_words.rearrange("g p n -> p g n").bitcast(I32)
-            )
+            loads = [(words[:, place:last, :].bitcast(I32), w_words.rearrange("g p n -> p g n").bitcast(I32))]
             for quad in range(4):
-                nc.sync.dma_start(
-                    out=planes[32 * quad : 32 * quad + 4, place:last, :].bitcast(I32),
-                    in_=w_scales[:, 4 * quad : 4 * quad + 4, :].rearrange("g r n -> r g n").bitcast(I32),
-                )
+                rows = w_scales[:, 4 * quad : 4 * quad + 4, :].rearrange("g r n -> r g n")
+                loads.append((planes[32 * quad : 32 * quad + 4, place:last, :].bitcast(I32), rows.bitcast(I32)))
+            return loads
 
-        def load_exchanged_weight(place, w_words, w_scales):
+        def exchanged_weight_loads(place, w_words, w_scales):
+            loads = []
             for h in range(2):
-                nc.sync.dma_start(
-                    out=words[h * HALF : (h + 1) * HALF, place, :].bitcast(I32),
-                    in_=w_words[0, (1 - h) * HALF : (2 - h) * HALF, :].bitcast(I32),
-                )
+                rows = w_words[0, (1 - h) * HALF : (2 - h) * HALF, :]
+                loads.append((words[h * HALF : (h + 1) * HALF, place, :].bitcast(I32), rows.bitcast(I32)))
             for quad in range(4):
                 row = 4 * ((quad + 2) % 4)
-                nc.sync.dma_start(
-                    out=planes[32 * quad : 32 * quad + 4, place, :].bitcast(I32),
-                    in_=w_scales[0, row : row + 4, :].bitcast(I32),
-                )
+                rows = w_scales[0, row : row + 4, :]
+                loads.append((planes[32 * quad : 32 * quad + 4, place, :].bitcast(I32), rows.bitcast(I32)))
+            return loads
 
         def block_and_electron(unit):
             return unit // UNITS_PER_BLOCK, PAIR * (unit % UNITS_PER_BLOCK)
@@ -99,7 +104,7 @@ def tile_ferminetoneelectronlayer_pa_t_kernel(
             nc.sync.dma_start(out=x1[:], in_=in_1e[blk * P : (blk + 1) * P])
             x1_of[blk] = x1
 
-        def load_two_electron(g):
+        def load_two_electron(g, between=()):
             blk, electron = block_and_electron(UNITS_PER_GROUP * g)
             ty = ty_pool.tile([P, PER_SPIN, PER_SPIN, SPINS, D2], BF16)
             for q in range(PER_SPIN):
@@ -114,24 +119,26 @@ def tile_ferminetoneelectronlayer_pa_t_kernel(
                             :,
                         ],
                     )
+                    for to, source in between[q * PER_SPIN + j : q * PER_SPIN + j + 1]:
+                        nc.sync.dma_start(out=to, in_=source)
             e2_of[g] = ty
 
-        def load_group(g):
-            if g % SPINS == 0:
-                load_one_electron(g // SPINS)
-            load_two_electron(g)
-
-        def sum_one_electron(blk, step):
-            if step == 0:
-                halves = x1_of[blk][:].rearrange("p (s h l) d -> p s h (l d)", s=SPINS, h=2, l=2)
-                m_half = work.tile([P, SPINS, 2 * D1], F32, bufs=1)
-                nc.vector.tensor_tensor(out=m_half[:], in0=halves[:, :, 0, :], in1=halves[:, :, 1, :], op=ADD)
+        def add_first_pairs(engine, blk, parts):
+            if parts[0] == 0:
+                m_half = work.tile([P, SPINS * 2, D1], F32, bufs=1)
                 sums_of["half", blk] = m_half
-            else:
-                m_sum = work.tile([P, SPINS, D1], BF16)
-                rest = sums_of["half", blk][:].rearrange("p s (l d) -> p s l d", l=2)
-                nc.vector.tensor_tensor(out=m_sum[:], in0=rest[:, :, 0, :], in1=rest[:, :, 1, :], op=ADD)
-                sums_of["m", blk] = m_sum
+            x1 = x1_of[blk]
+            for part in parts:
+                i = PER_SPIN * (part // 2) + part % 2
+                engine.tensor_tensor(
+                    out=sums_of["half", blk][:, part, :], in0=x1[:, i, :], in1=x1[:, i + 2, :], op=ADD
+                )
+
+        def add_second_pairs(blk):
+            m_sum = work.tile([P, SPINS, D1], BF16)
+            halves = sums_of["half", blk][:].rearrange("p (s l) d -> p s l d", l=2)
+            nc.vector.tensor_tensor(out=m_sum[:], in0=halves[:, :, 0, :], in1=halves[:, :, 1, :], op=ADD)
+            sums_of["m", blk] = m_sum
 
         def transpose_rows(rows):
             as_words = rows.bitcast(F32)
@@ -144,7 +151,6 @@ def tile_ferminetoneelectronlayer_pa_t_kernel(
         def average_two_electron(unit):
             first = PAIR * (unit % UNITS_PER_GROUP)
             features = e2_of[unit // UNITS_PER_GROUP][:].rearrange("p q i s d -> p q i (s d)")
-            a_grouped = work.tile([P, PAIR, P, PACK], BF16, align_bytes=64, bufs=3)
             bank = tp_pool.tile([P, PAIR, PACK, P], BF16, tag="tp")
             for q in range(PER_SPIN):
                 for e in range(PAIR):
@@ -156,17 +162,16 @@ def tile_ferminetoneelectronlayer_pa_t_kernel(
                             start=True,
                             stop=True,
                         )
-            nc.scalar.copy(out=a_grouped[:], in_=bank[:].rearrange("p e t w -> p e w t"))
-            grouped_of["a", unit] = a_grouped
+            nc.scalar.copy(out=grouped_of["xa", unit][:, PAIR:], in_=bank[:].rearrange("p e t w -> p e w t"))
 
         def transpose_inputs(unit):
             blk, electron = block_and_electron(unit)
             bank = transpose_rows(x1_of[blk][:, electron : electron + PAIR, :])
-            x_grouped = work.tile([P, PAIR, P, PACK], BF16, align_bytes=64)
-            x_words = x_grouped[:].rearrange("p i w t -> p (i w t)").bitcast(F32)
+            xa_grouped = work.tile([P, 2 * PAIR, P, PACK], BF16, align_bytes=64, bufs=3)
+            x_words = xa_grouped[:, 0:PAIR].rearrange("p i w t -> p (i w t)").bitcast(F32)
             x_words = x_words.rearrange("p (i w u) -> p i w u", i=PAIR, w=P, u=2)
             nc.scalar.copy(out=x_words, in_=bank[:].rearrange("p (r u) w -> p r w u", u=2))
-            grouped_of["x", unit] = x_grouped
+            grouped_of["xa", unit] = xa_grouped
 
         def transpose_one_electron_sums(blk):
             bank = transpose_rows(sums_of["m", blk][:])
@@ -182,10 +187,10 @@ def tile_ferminetoneelectronlayer_pa_t_kernel(
                 )
             grouped_of["m", blk] = m_grouped
 
-        def quantise(key):
+        def quantise(key, count):
             grouped = grouped_of[key]
-            codes = work.tile([P, 2, P], U32, align_bytes=64, tag="codes_" + key[0])
-            scales = work.tile([P, 2, P], U8, align_bytes=64, tag="scales_" + key[0])
+            codes = work.tile([P, count, P], U32, align_bytes=64, tag="codes_" + key[0])
+            scales = work.tile([P, count, P], U8, align_bytes=64, tag="scales_" + key[0])
             nc.vector.quantize_mx(
                 out=codes[:].rearrange("p i w -> p (i w)").bitcast(FP8X4),
                 scales=scales[:].rearrange("p i w -> p (i w)"),
@@ -195,9 +200,8 @@ def tile_ferminetoneelectronlayer_pa_t_kernel(
 
         def quantise_unit(unit):
             if unit % UNITS_PER_BLOCK == 0:
-                quantise(("m", unit // UNITS_PER_BLOCK))
-            quantise(("x", unit))
-            quantise(("a", unit))
+                quantise(("m", unit // UNITS_PER_BLOCK), SPINS)
+            quantise(("xa", unit), 2 * PAIR)
 
         def mx_pass(acc, key, row, place, start, stop):
             codes, scales = codes_of[key]
@@ -223,8 +227,8 @@ def tile_ferminetoneelectronlayer_pa_t_kernel(
                 gb_of[blk] = gb
             for i in range(PAIR):
                 acc = acc_pool.tile([P, D1], F32, tag="acc")
-                mx_pass(acc, ("x", unit), i, W_U, True, False)
-                mx_pass(acc, ("a", unit), i, W_E + electron // PER_SPIN, False, True)
+                mx_pass(acc, ("xa", unit), i, W_U, True, False)
+                mx_pass(acc, ("xa", unit), PAIR + i, W_E + electron // PER_SPIN, False, True)
                 acc_of[unit, i] = acc
 
         def leave_psum(unit):
@@ -246,20 +250,24 @@ def tile_ferminetoneelectronlayer_pa_t_kernel(
         def is_unit(unit):
             return 0 <= unit < UNITS
 
-        load_group(0)
-        load_weight(W_M_OWN, wm_words, wm_scales)
-        load_weight(W_U, wu_words, wu_scales)
-        load_weight(W_E, w2_words, w2_scales)
-        nc.sync.dma_start(out=bias_bc[:], in_=b_unmixed.partition_broadcast(P))
-        load_group(1)
-        load_exchanged_weight(W_E + 1, w2_words, w2_scales)
+        load_one_electron(0)
+        load_two_electron(
+            0,
+            weight_loads(W_M_OWN, wm_words, wm_scales)
+            + weight_loads(W_U, wu_words, wu_scales)
+            + weight_loads(W_E, w2_words, w2_scales),
+        )
+        load_two_electron(1, exchanged_weight_loads(W_E + 1, w2_words, w2_scales))
+        load_one_electron(1)
         for g in range(2, GROUPS_AHEAD):
-            load_group(g)
+            load_two_electron(g)
+            if g % SPINS:
+                load_one_electron(g // SPINS + 1)
         for n in range(-2, UNITS + 3):
-            if is_unit(n):
-                transpose_inputs(n)
-                if n % UNITS_PER_BLOCK == 0:
-                    transpose_one_electron_sums(n // UNITS_PER_BLOCK)
+            if is_unit(n + 1):
+                transpose_inputs(n + 1)
+            if n == -1 or (is_unit(n) and n > 0 and n % UNITS_PER_BLOCK == 0):
+                transpose_one_electron_sums(max(n, 0) // UNITS_PER_BLOCK)
             if is_unit(n - 1):
                 quantise_unit(n - 1)
             if is_unit(n - 2):
@@ -268,11 +276,16 @@ def tile_ferminetoneelectronlayer_pa_t_kernel(
                 multiply_unit(n - 1)
             if is_unit(n - 3):
                 finish_unit(n - 3)
-            for step in range(2):
-                if is_unit(n + 2 - step) and (n + 2 - step) % UNITS_PER_BLOCK == 0:
-                    sum_one_electron((n + 2 - step) // UNITS_PER_BLOCK, step)
+            if n == -2:
+                add_first_pairs(nc.vector, 0, range(2 * SPINS))
+                add_second_pairs(0)
+            nearest = (n + 1) // UNITS_PER_BLOCK
+            if n > 0 and (n + 1) % UNITS_PER_BLOCK == 0 and nearest < BLOCKS:
+                add_second_pairs(nearest)
+            if n >= -1 and nearest + 1 < BLOCKS:
+                add_first_pairs(nc.gpsimd, nearest + 1, [(n + 1) % UNITS_PER_BLOCK])
             if is_unit(n + 1):
                 average_two_electron(n + 1)
             ahead = n // UNITS_PER_GROUP + GROUPS_AHEAD
             if n >= 0 and n % UNITS_PER_GROUP == 0 and ahead < GROUPS:
-                load_group(ahead)
+                load_two_electron(ahead)

@@ -27,6 +27,7 @@ UNITS_PER_GROUP = PER_SPIN // PAIR
 UNITS_PER_BLOCK = UNITS_PER_GROUP * SPINS
 UNITS = GROUPS * UNITS_PER_GROUP
 OUT_TILES = 12
+WALKER_GROUPS = (0,)
 GROUPS_AHEAD = 6
 QUARTER = P // PER_SPIN
 
@@ -68,12 +69,14 @@ def tile_ferminetoneelectronlayer_pa_t_kernel(
         nc.vector.tensor_copy(out=ident_bf16[:], in_=ident[:])
         bias_col = const.tile([P, PACK], BF16)
         nc.gpsimd.dma_start(out=bias_col[:], in_=b_unmixed.rearrange("(p t) -> p t", t=PACK))
-        bias_bank = tp_pool.tile([P, PACK, P], BF16, tag="tp")
-        for t in range(PACK):
-            nc.tensor.transpose(bias_bank[:, t, :], bias_col[:, t : t + 1].to_broadcast([P, P]), ident_bf16[:])
-        nc.scalar.copy(
-            out=bias_bc[:].rearrange("p (k t) -> p k t", t=PACK), in_=bias_bank[:].rearrange("p t k -> p k t")
-        )
+
+        def spread_bias():
+            bias_bank = tp_pool.tile([P, PACK, P], BF16, tag="tp")
+            for t in range(PACK):
+                nc.tensor.transpose(bias_bank[:, t, :], bias_col[:, t : t + 1].to_broadcast([P, P]), ident_bf16[:])
+            nc.scalar.copy(
+                out=bias_bc[:].rearrange("p (k t) -> p k t", t=PACK), in_=bias_bank[:].rearrange("p t k -> p k t")
+            )
 
         def weight_loads(place, w_words, w_scales):
             last = place + w_words.shape[0]
@@ -104,9 +107,24 @@ def tile_ferminetoneelectronlayer_pa_t_kernel(
             nc.sync.dma_start(out=x1[:], in_=in_1e[blk * P : (blk + 1) * P])
             x1_of[blk] = x1
 
+        def load_small(loads):
+            for to, source in loads:
+                nc.sync.dma_start(out=to, in_=source)
+
+        def load_by_walker(unit):
+            blk, electron = block_and_electron(unit)
+            first = electron % PER_SPIN
+            if first == 0:
+                rows = ty_pool.tile([P, PER_SPIN, SPINS, PER_SPIN, D2], BF16, tag="ty")
+                e2_of[unit // UNITS_PER_GROUP] = rows
+            nc.sync.dma_start(
+                out=e2_of[unit // UNITS_PER_GROUP][:, first : first + PAIR].rearrange("p i s j d -> p i (s j) d"),
+                in_=in_2e[blk * P : (blk + 1) * P, electron : electron + PAIR],
+            )
+
         def load_two_electron(g, between=()):
             blk, electron = block_and_electron(UNITS_PER_GROUP * g)
-            ty = ty_pool.tile([P, PER_SPIN, PER_SPIN, SPINS, D2], BF16)
+            ty = ty_pool.tile([P, PER_SPIN, PER_SPIN, SPINS, D2], BF16, tag="ty")
             for q in range(PER_SPIN):
                 first_walker = blk * P + q * QUARTER
                 for j in range(PER_SPIN):
@@ -119,8 +137,7 @@ def tile_ferminetoneelectronlayer_pa_t_kernel(
                             :,
                         ],
                     )
-                    for to, source in between[q * PER_SPIN + j : q * PER_SPIN + j + 1]:
-                        nc.sync.dma_start(out=to, in_=source)
+                    load_small(between[q * PER_SPIN + j : q * PER_SPIN + j + 1])
             e2_of[g] = ty
 
         def add_first_pairs(engine, blk, parts):
@@ -135,10 +152,25 @@ def tile_ferminetoneelectronlayer_pa_t_kernel(
                 )
 
         def add_second_pairs(blk):
-            m_sum = work.tile([P, SPINS, D1], BF16)
+            m_sum = work.tile([P, SPINS, D1], BF16, bufs=1)
             halves = sums_of["half", blk][:].rearrange("p (s l) d -> p s l d", l=2)
             nc.vector.tensor_tensor(out=m_sum[:], in0=halves[:, :, 0, :], in1=halves[:, :, 1, :], op=ADD)
             sums_of["m", blk] = m_sum
+
+        def add_partners(unit):
+            first = PAIR * (unit % UNITS_PER_GROUP)
+            halves = e2_of[unit // UNITS_PER_GROUP][:, first : first + PAIR].rearrange("p i s (h l) d -> p (i s) h (l d)", h=2)
+            a_half = work.tile([P, PAIR * SPINS, 2 * D2], F32, bufs=1)
+            nc.vector.tensor_tensor(out=a_half[:], in0=halves[:, :, 0, :], in1=halves[:, :, 1, :], op=ADD)
+            a_sum = work.tile([P, PAIR, SPINS * D2], BF16)
+            rest = a_half[:].rearrange("p n (l d) -> p n l d", l=2)
+            nc.vector.tensor_tensor(
+                out=a_sum[:].rearrange("p i (s d) -> p (i s) d", s=SPINS),
+                in0=rest[:, :, 0, :],
+                in1=rest[:, :, 1, :],
+                op=ADD,
+            )
+            sums_of["a", unit] = a_sum
 
         def transpose_rows(rows):
             as_words = rows.bitcast(F32)
@@ -173,24 +205,28 @@ def tile_ferminetoneelectronlayer_pa_t_kernel(
             nc.scalar.copy(out=x_words, in_=bank[:].rearrange("p (r u) w -> p r w u", u=2))
             grouped_of["xa", unit] = xa_grouped
 
-        def transpose_one_electron_sums(blk):
-            bank = transpose_rows(sums_of["m", blk][:])
-            m_grouped = work.tile([P, SPINS, P, PACK], BF16, align_bytes=64)
+        def transpose_sums(sums, grouped):
+            bank = transpose_rows(sums)
             values = bank[:].rearrange("p a w -> p (a w)").bitcast(BF16)
             values = values.rearrange("p (r u w e) -> p r w u e", r=2, u=2, w=P, e=2)
-            for s in range(SPINS):
+            for r in range(2):
                 nc.scalar.activation(
-                    out=m_grouped[:, s, :, :].rearrange("p w (u e) -> p w u e", u=2),
-                    in_=values[:, s],
+                    out=grouped[:, r, :, :].rearrange("p w (u e) -> p w u e", u=2),
+                    in_=values[:, r],
                     func=ACT.Copy,
                     scale=1.0 / PER_SPIN,
                 )
+
+        def transpose_one_electron_sums(blk):
+            m_grouped = work.tile([P, SPINS, P, PACK], BF16, align_bytes=64, bufs=1)
+            transpose_sums(sums_of["m", blk][:], m_grouped)
             grouped_of["m", blk] = m_grouped
 
         def quantise(key, count):
             grouped = grouped_of[key]
-            codes = work.tile([P, count, P], U32, align_bytes=64, tag="codes_" + key[0])
-            scales = work.tile([P, count, P], U8, align_bytes=64, tag="scales_" + key[0])
+            bufs = 1 if key[0] == "m" else 2
+            codes = work.tile([P, count, P], U32, align_bytes=64, tag="codes_" + key[0], bufs=bufs)
+            scales = work.tile([P, count, P], U8, align_bytes=64, tag="scales_" + key[0], bufs=bufs)
             nc.vector.quantize_mx(
                 out=codes[:].rearrange("p i w -> p (i w)").bitcast(FP8X4),
                 scales=scales[:].rearrange("p i w -> p (i w)"),
@@ -247,27 +283,36 @@ def tile_ferminetoneelectronlayer_pa_t_kernel(
             nc.vector.tensor_tensor(out=o[:], in0=o[:], in1=x1_of[blk][:, electron : electron + PAIR, :], op=ADD)
             nc.sync.dma_start(out=out[blk * P : (blk + 1) * P, electron : electron + PAIR, :], in_=o[:])
 
+        def by_walker(unit):
+            return unit // UNITS_PER_GROUP in WALKER_GROUPS
+
+        def load_group(g, between=()):
+            if g in WALKER_GROUPS:
+                for unit in range(UNITS_PER_GROUP * g, UNITS_PER_GROUP * (g + 1)):
+                    load_by_walker(unit)
+            else:
+                load_two_electron(g, between)
+            if g % SPINS and g // SPINS + 1 < BLOCKS:
+                load_one_electron(g // SPINS + 1)
+
         def is_unit(unit):
             return 0 <= unit < UNITS
 
         load_one_electron(0)
-        load_two_electron(
-            0,
-            weight_loads(W_M_OWN, wm_words, wm_scales)
-            + weight_loads(W_U, wu_words, wu_scales)
-            + weight_loads(W_E, w2_words, w2_scales),
-        )
-        load_two_electron(1, exchanged_weight_loads(W_E + 1, w2_words, w2_scales))
-        load_one_electron(1)
+        load_by_walker(0)
+        load_small(weight_loads(W_M_OWN, wm_words, wm_scales))
+        load_by_walker(1)
+        load_small(weight_loads(W_U, wu_words, wu_scales) + weight_loads(W_E, w2_words, w2_scales))
+        load_group(1, exchanged_weight_loads(W_E + 1, w2_words, w2_scales))
         for g in range(2, GROUPS_AHEAD):
-            load_two_electron(g)
-            if g % SPINS:
-                load_one_electron(g // SPINS + 1)
+            load_group(g)
         for n in range(-2, UNITS + 3):
             if is_unit(n + 1):
                 transpose_inputs(n + 1)
             if n == -1 or (is_unit(n) and n > 0 and n % UNITS_PER_BLOCK == 0):
                 transpose_one_electron_sums(max(n, 0) // UNITS_PER_BLOCK)
+            if n == 0:
+                spread_bias()
             if is_unit(n - 1):
                 quantise_unit(n - 1)
             if is_unit(n - 2):
@@ -284,8 +329,13 @@ def tile_ferminetoneelectronlayer_pa_t_kernel(
                 add_second_pairs(nearest)
             if n >= -1 and nearest + 1 < BLOCKS:
                 add_first_pairs(nc.gpsimd, nearest + 1, [(n + 1) % UNITS_PER_BLOCK])
+            if is_unit(n + 2) and by_walker(n + 2):
+                add_partners(n + 2)
             if is_unit(n + 1):
-                average_two_electron(n + 1)
+                if by_walker(n + 1):
+                    transpose_sums(sums_of["a", n + 1][:], grouped_of["xa", n + 1][:, PAIR:])
+                else:
+                    average_two_electron(n + 1)
             ahead = n // UNITS_PER_GROUP + GROUPS_AHEAD
             if n >= 0 and n % UNITS_PER_GROUP == 0 and ahead < GROUPS:
-                load_two_electron(ahead)
+                load_group(ahead)

@@ -26,9 +26,9 @@ PAIR = 2
 UNITS_PER_GROUP = PER_SPIN // PAIR
 UNITS_PER_BLOCK = UNITS_PER_GROUP * SPINS
 UNITS = GROUPS * UNITS_PER_GROUP
-OUT_TILES = 12
+OUT_TILES = 16
 WALKER_GROUPS = (0,)
-GROUPS_AHEAD = 6
+GROUPS_AHEAD = 5
 QUARTER = P // PER_SPIN
 
 W_U, W_M_OWN, W_M_OTHER, W_E = 0, 1, 2, 3
@@ -137,7 +137,8 @@ def tile_ferminetoneelectronlayer_pa_t_kernel(
                             :,
                         ],
                     )
-                    load_small(between[q * PER_SPIN + j : q * PER_SPIN + j + 1])
+                    if q * PER_SPIN + j < len(between):
+                        load_small(between[q * PER_SPIN + j])
             e2_of[g] = ty
 
         def add_first_pairs(engine, blk, parts):
@@ -235,8 +236,6 @@ def tile_ferminetoneelectronlayer_pa_t_kernel(
             codes_of[key] = (codes, scales)
 
         def quantise_unit(unit):
-            if unit % UNITS_PER_BLOCK == 0:
-                quantise(("m", unit // UNITS_PER_BLOCK), SPINS)
             quantise(("xa", unit), 2 * PAIR)
 
         def mx_pass(acc, key, row, place, start, stop):
@@ -251,16 +250,21 @@ def tile_ferminetoneelectronlayer_pa_t_kernel(
                 stop=stop,
             )
 
+        def multiply_means(blk):
+            for s in range(SPINS):
+                acc_g = acc_pool.tile([P, D1], F32, tag="acc")
+                mx_pass(acc_g, ("m", blk), s, W_M_OWN, True, False)
+                mx_pass(acc_g, ("m", blk), 1 - s, W_M_OTHER, False, True)
+                acc_of["g", blk, s] = acc_g
+
+        def add_bias(blk):
+            gb = work.tile([P, SPINS, D1], F32)
+            for s in range(SPINS):
+                nc.vector.tensor_tensor(out=gb[:, s, :], in0=acc_of["g", blk, s][:], in1=bias_bc[:], op=ADD)
+            gb_of[blk] = gb
+
         def multiply_unit(unit):
             blk, electron = block_and_electron(unit)
-            if unit % UNITS_PER_BLOCK == 0:
-                gb = work.tile([P, SPINS, D1], F32)
-                for s in range(SPINS):
-                    acc_g = acc_pool.tile([P, D1], F32, tag="acc")
-                    mx_pass(acc_g, ("m", blk), s, W_M_OWN, True, False)
-                    mx_pass(acc_g, ("m", blk), 1 - s, W_M_OTHER, False, True)
-                    nc.vector.tensor_tensor(out=gb[:, s, :], in0=acc_g[:], in1=bias_bc[:], op=ADD)
-                gb_of[blk] = gb
             for i in range(PAIR):
                 acc = acc_pool.tile([P, D1], F32, tag="acc")
                 mx_pass(acc, ("xa", unit), i, W_U, True, False)
@@ -277,11 +281,15 @@ def tile_ferminetoneelectronlayer_pa_t_kernel(
             nc.scalar.activation(out=o[:], in_=o[:], func=ACT.Tanh)
             o_of[unit] = o
 
+        def store_unit(unit):
+            blk, electron = block_and_electron(unit)
+            nc.sync.dma_start(out=out[blk * P : (blk + 1) * P, electron : electron + PAIR, :], in_=o_of[unit][:])
+
         def finish_unit(unit):
             blk, electron = block_and_electron(unit)
             o = o_of[unit]
             nc.vector.tensor_tensor(out=o[:], in0=o[:], in1=x1_of[blk][:, electron : electron + PAIR, :], op=ADD)
-            nc.sync.dma_start(out=out[blk * P : (blk + 1) * P, electron : electron + PAIR, :], in_=o[:])
+
 
         def by_walker(unit):
             return unit // UNITS_PER_GROUP in WALKER_GROUPS
@@ -292,43 +300,72 @@ def tile_ferminetoneelectronlayer_pa_t_kernel(
                     load_by_walker(unit)
             else:
                 load_two_electron(g, between)
-            if g % SPINS and g // SPINS + 1 < BLOCKS:
+            if g % SPINS == 0 and g and g // SPINS + 1 < BLOCKS:
                 load_one_electron(g // SPINS + 1)
 
         def is_unit(unit):
             return 0 <= unit < UNITS
 
+        def sparse(loads, every):
+            out_list = []
+            for load in loads:
+                out_list += [()] * (every - 1) + [(load,)]
+            return out_list
+
         load_one_electron(0)
-        load_by_walker(0)
         load_small(weight_loads(W_M_OWN, wm_words, wm_scales))
+        load_by_walker(0)
+        load_small(weight_loads(W_U, wu_words, wu_scales))
         load_by_walker(1)
-        load_small(weight_loads(W_U, wu_words, wu_scales) + weight_loads(W_E, w2_words, w2_scales))
-        load_group(1, exchanged_weight_loads(W_E + 1, w2_words, w2_scales))
+        load_small(weight_loads(W_E, w2_words, w2_scales))
+        load_one_electron(1)
+        load_two_electron(1, sparse(exchanged_weight_loads(W_E + 1, w2_words, w2_scales), 2))
         for g in range(2, GROUPS_AHEAD):
             load_group(g)
+        def block_at(n, offset):
+            first = n + offset
+            if first % UNITS_PER_BLOCK == 0 and 0 <= first // UNITS_PER_BLOCK < BLOCKS:
+                return first // UNITS_PER_BLOCK
+            return None
+        finished = []
         for n in range(-2, UNITS + 3):
+            if n == -2:
+                add_first_pairs(nc.vector, 0, range(2 * SPINS))
+                add_second_pairs(0)
             if is_unit(n + 1):
                 transpose_inputs(n + 1)
-            if n == -1 or (is_unit(n) and n > 0 and n % UNITS_PER_BLOCK == 0):
-                transpose_one_electron_sums(max(n, 0) // UNITS_PER_BLOCK)
+            if n == -2:
+                transpose_one_electron_sums(0)
+            b = block_at(n, 1)
+            if b:
+                transpose_one_electron_sums(b)
             if n == 0:
                 spread_bias()
+            b = block_at(n, 0)
+            if b is not None:
+                quantise(("m", b), SPINS)
             if is_unit(n - 1):
                 quantise_unit(n - 1)
+            b = block_at(n, -1)
+            if b is not None:
+                add_bias(b)
             if is_unit(n - 2):
                 leave_psum(n - 2)
             if is_unit(n - 1):
                 multiply_unit(n - 1)
+            b = block_at(n, 0)
+            if b is not None:
+                multiply_means(b)
             if is_unit(n - 3):
                 finish_unit(n - 3)
-            if n == -2:
-                add_first_pairs(nc.vector, 0, range(2 * SPINS))
-                add_second_pairs(0)
-            nearest = (n + 1) // UNITS_PER_BLOCK
-            if n > 0 and (n + 1) % UNITS_PER_BLOCK == 0 and nearest < BLOCKS:
-                add_second_pairs(nearest)
-            if n >= -1 and nearest + 1 < BLOCKS:
-                add_first_pairs(nc.gpsimd, nearest + 1, [(n + 1) % UNITS_PER_BLOCK])
+                finished.append(n - 3)
+            b = block_at(n, 2)
+            if b:
+                add_second_pairs(b)
+            if n >= -2:
+                b = (n + 6) // UNITS_PER_BLOCK
+                if 1 <= b < BLOCKS:
+                    add_first_pairs(nc.gpsimd, b, [(n + 2) % UNITS_PER_BLOCK])
             if is_unit(n + 2) and by_walker(n + 2):
                 add_partners(n + 2)
             if is_unit(n + 1):
@@ -339,3 +376,5 @@ def tile_ferminetoneelectronlayer_pa_t_kernel(
             ahead = n // UNITS_PER_GROUP + GROUPS_AHEAD
             if n >= 0 and n % UNITS_PER_GROUP == 0 and ahead < GROUPS:
                 load_group(ahead)
+            while finished and n >= UNITS_PER_GROUP * (GROUPS - 1 - GROUPS_AHEAD):
+                store_unit(finished.pop(0))

@@ -27,7 +27,7 @@ UNITS_PER_GROUP = PER_SPIN // PAIR
 UNITS_PER_BLOCK = UNITS_PER_GROUP * SPINS
 UNITS = GROUPS * UNITS_PER_GROUP
 OUT_TILES = 16
-WALKER_GROUPS = (0,)
+WALKER_GROUPS = (0, 1)
 GROUPS_AHEAD = 5
 QUARTER = P // PER_SPIN
 
@@ -65,6 +65,8 @@ def tile_ferminetoneelectronlayer_pa_t_kernel(
         )
         averager = const.tile([P, QUARTER], BF16)
         nc.scalar.activation(out=averager[:], in_=fours[:], func=ACT.Copy, scale=1.0 / PER_SPIN)
+        quarter = const.tile([P, P], BF16)
+        nc.scalar.activation(out=quarter[:], in_=ident[:], func=ACT.Copy, scale=1.0 / PER_SPIN)
         ident_bf16 = const.tile([P, P], BF16)
         nc.vector.tensor_copy(out=ident_bf16[:], in_=ident[:])
         bias_col = const.tile([P, PACK], BF16)
@@ -219,8 +221,24 @@ def tile_ferminetoneelectronlayer_pa_t_kernel(
                 )
 
         def transpose_one_electron_sums(blk):
-            m_grouped = work.tile([P, SPINS, P, PACK], BF16, align_bytes=64, bufs=1)
+            m_grouped = work.tile([P, SPINS, P, PACK], BF16, align_bytes=64, tag="m_grouped", bufs=1)
             transpose_sums(sums_of["m", blk][:], m_grouped)
+            grouped_of["m", blk] = m_grouped
+
+        def average_one_electron(blk):
+            m_grouped = work.tile([P, SPINS, P, PACK], BF16, align_bytes=64, tag="m_grouped", bufs=1)
+            for s in range(SPINS):
+                bank = tp_pool.tile([P, PACK, P], F32, tag="tp")
+                for t in range(PACK):
+                    for i in range(PER_SPIN):
+                        nc.tensor.matmul(
+                            out=bank[:, t, :],
+                            lhsT=x1_of[blk][:, PER_SPIN * s + i, t:D1:PACK],
+                            rhs=quarter[:],
+                            start=i == 0,
+                            stop=i == PER_SPIN - 1,
+                        )
+                nc.scalar.copy(out=m_grouped[:, s], in_=bank[:].rearrange("p t w -> p w t"))
             grouped_of["m", blk] = m_grouped
 
         def quantise(key, count):
@@ -312,14 +330,16 @@ def tile_ferminetoneelectronlayer_pa_t_kernel(
                 out_list += [()] * (every - 1) + [(load,)]
             return out_list
 
+        load_by_walker(0)
         load_one_electron(0)
         load_small(weight_loads(W_M_OWN, wm_words, wm_scales))
-        load_by_walker(0)
-        load_small(weight_loads(W_U, wu_words, wu_scales))
         load_by_walker(1)
+        load_small(weight_loads(W_U, wu_words, wu_scales))
+        load_by_walker(2)
         load_small(weight_loads(W_E, w2_words, w2_scales))
+        load_by_walker(3)
+        load_small(exchanged_weight_loads(W_E + 1, w2_words, w2_scales))
         load_one_electron(1)
-        load_two_electron(1, sparse(exchanged_weight_loads(W_E + 1, w2_words, w2_scales), 2))
         for g in range(2, GROUPS_AHEAD):
             load_group(g)
         def block_at(n, offset):
@@ -329,13 +349,10 @@ def tile_ferminetoneelectronlayer_pa_t_kernel(
             return None
         finished = []
         for n in range(-2, UNITS + 3):
-            if n == -2:
-                add_first_pairs(nc.vector, 0, range(2 * SPINS))
-                add_second_pairs(0)
             if is_unit(n + 1):
                 transpose_inputs(n + 1)
             if n == -2:
-                transpose_one_electron_sums(0)
+                average_one_electron(0)
             b = block_at(n, 1)
             if b:
                 transpose_one_electron_sums(b)

@@ -26,7 +26,8 @@ PAIR = 2
 UNITS_PER_GROUP = PER_SPIN // PAIR
 UNITS_PER_BLOCK = UNITS_PER_GROUP * SPINS
 UNITS = GROUPS * UNITS_PER_GROUP
-OUT_TILES = 16
+OUT_TILES = GROUPS
+LAST = UNITS - 1
 WALKER_GROUPS = (0, 1)
 GROUPS_AHEAD = 5
 QUARTER = P // PER_SPIN
@@ -127,20 +128,28 @@ def tile_ferminetoneelectronlayer_pa_t_kernel(
         def load_two_electron(g, between=()):
             blk, electron = block_and_electron(UNITS_PER_GROUP * g)
             ty = ty_pool.tile([P, PER_SPIN, PER_SPIN, SPINS, D2], BF16, tag="ty")
+            all_partners = SPINS * PER_SPIN
+            first_row, last_row = electron * all_partners, (electron + PER_SPIN) * all_partners - 1
+            by_quarter = in_2e[blk * P : (blk + 1) * P].rearrange("(q w) i j d -> w q (i j) d", q=PER_SPIN)
+            every_slot = ty[:].rearrange("p q i s d -> p q (i s) d")
+            nc.sync.dma_start(out=every_slot[0:P:PER_SPIN, :, 0], in_=by_quarter[:, :, first_row])
+            nc.sync.dma_start(out=every_slot[0:P:PER_SPIN, :, SPINS * PER_SPIN - 1], in_=by_quarter[:, :, last_row])
             for q in range(PER_SPIN):
-                first_walker = blk * P + q * QUARTER
-                for j in range(PER_SPIN):
-                    nc.sync.dma_start(
-                        out=ty[j:P:PER_SPIN, q],
-                        in_=in_2e[
-                            first_walker : first_walker + QUARTER,
-                            electron : electron + PER_SPIN,
-                            j : SPINS * PER_SPIN : PER_SPIN,
-                            :,
-                        ],
-                    )
-                    if q * PER_SPIN + j < len(between):
-                        load_small(between[q * PER_SPIN + j])
+                walkers = slice(blk * P + q * QUARTER, blk * P + (q + 1) * QUARTER)
+                rows = in_2e[walkers].rearrange("w i j d -> w (i j) d")
+                slots = ty[:, q].rearrange("p i s d -> p (i s) d")
+                inner = rows[:, first_row + all_partners - 1 : last_row].rearrange("w (m r) d -> w m r d", r=all_partners)
+                pairs = slots[0:P:PER_SPIN, 1 : SPINS * PER_SPIN - 1].rearrange("p (m r) d -> p m r d", r=SPINS)
+                loads = [
+                    (ty[1:P:PER_SPIN, q], in_2e[walkers, electron : electron + PER_SPIN, 1:all_partners:PER_SPIN, :]),
+                    (ty[2:P:PER_SPIN, q], in_2e[walkers, electron : electron + PER_SPIN, 2:all_partners:PER_SPIN, :]),
+                    (ty[3:P:PER_SPIN, q], in_2e[walkers, electron : electron + PER_SPIN, 3:5, :]),
+                    (pairs, inner[:, :, 0:SPINS, :]),
+                ]
+                for number, (to, source) in enumerate(loads):
+                    nc.sync.dma_start(out=to, in_=source)
+                    if q * PER_SPIN + number < len(between):
+                        load_small(between[q * PER_SPIN + number])
             e2_of[g] = ty
 
         def add_first_pairs(engine, blk, parts):
@@ -291,22 +300,43 @@ def tile_ferminetoneelectronlayer_pa_t_kernel(
 
         def leave_psum(unit):
             blk, electron = block_and_electron(unit)
-            o = out_pool.tile([P, PAIR, D1], F32)
+            g, first = unit // UNITS_PER_GROUP, electron % PER_SPIN
+            if first == 0:
+                group_out = out_pool.tile([P, PER_SPIN, D1], F32)
+                o_of["group", g] = group_out
+            o = o_of["group", g][:, first : first + PAIR, :]
             for i in range(PAIR):
                 nc.vector.tensor_tensor(
                     out=o[:, i, :], in0=acc_of[unit, i][:], in1=gb_of[blk][:, electron // PER_SPIN, :], op=ADD
                 )
-            nc.scalar.activation(out=o[:], in_=o[:], func=ACT.Tanh)
+                if unit == LAST:
+                    nc.scalar.activation(out=o[:, i, :], in_=o[:, i, :], func=ACT.Tanh)
+            if unit != LAST:
+                nc.scalar.activation(out=o, in_=o, func=ACT.Tanh)
             o_of[unit] = o
 
         def store_unit(unit):
             blk, electron = block_and_electron(unit)
-            nc.sync.dma_start(out=out[blk * P : (blk + 1) * P, electron : electron + PAIR, :], in_=o_of[unit][:])
+            g = unit // UNITS_PER_GROUP
+            walkers = slice(blk * P, (blk + 1) * P)
+            if unit == LAST:
+                for i in range(PAIR):
+                    nc.sync.dma_start(out=out[walkers, electron + i, :], in_=o_of[unit][:, i, :])
+            elif g == GROUPS - 1:
+                nc.sync.dma_start(out=out[walkers, electron : electron + PAIR, :], in_=o_of[unit])
+            elif electron % PER_SPIN:
+                first = electron - PAIR
+                nc.sync.dma_start(out=out[walkers, first : first + PER_SPIN, :], in_=o_of["group", g][:])
 
         def finish_unit(unit):
             blk, electron = block_and_electron(unit)
             o = o_of[unit]
-            nc.vector.tensor_tensor(out=o[:], in0=o[:], in1=x1_of[blk][:, electron : electron + PAIR, :], op=ADD)
+            x1 = x1_of[blk][:, electron : electron + PAIR, :]
+            if unit == LAST:
+                for i in range(PAIR):
+                    nc.vector.tensor_tensor(out=o[:, i, :], in0=o[:, i, :], in1=x1[:, i, :], op=ADD)
+            else:
+                nc.vector.tensor_tensor(out=o, in0=o, in1=x1, op=ADD)
 
 
         def by_walker(unit):

from contextlib import ExitStack

import concourse.mybir as mybir
from concourse.masks import make_identity

F32 = mybir.dt.float32
BF16 = mybir.dt.bfloat16
I32 = mybir.dt.int32
U32 = mybir.dt.uint32
U8 = mybir.dt.uint8
FP8X4 = mybir.dt.float8_e4m3fn_x4
FP4X4 = mybir.dt.float4_e2m1fn_x4
ADD = mybir.AluOpType.add
ACT = mybir.ActivationFunctionType

P = 128
WALKERS = 512
SPINS = 2
PER_SPIN = 4
D1 = 512
D2 = 256
PACK = 4
BLOCKS = WALKERS // P
GROUPS = BLOCKS * SPINS
PAIR = 2
UNITS_PER_GROUP = PER_SPIN // PAIR
UNITS_PER_BLOCK = UNITS_PER_GROUP * SPINS
UNITS = GROUPS * UNITS_PER_GROUP
OUT_TILES = GROUPS
LAST = UNITS - 1
WALKER_GROUPS = (0, 1)
GROUPS_AHEAD = 5
QUARTER = P // PER_SPIN

W_U, W_M_OWN, W_M_OTHER, W_E = 0, 1, 2, 3
N_PASSES = 5
HALF = P // 2

FLOPS = 2 * WALKERS * 8 * D1 * D1 * 2 + 2 * WALKERS * SPINS * (SPINS * D1) * D1


def tile_ferminetoneelectronlayer_pa_t_kernel(
    tc, in_1e, in_2e, wu_words, wu_scales, b_unmixed, wm_words, wm_scales, w2_words, w2_scales, out
):
    nc = tc.nc
    with ExitStack() as ctx:
        const = ctx.enter_context(tc.tile_pool(name="const", bufs=1))
        x1_pool = ctx.enter_context(tc.tile_pool(name="x1", bufs=BLOCKS))
        ty_pool = ctx.enter_context(tc.tile_pool(name="ty", bufs=GROUPS_AHEAD))
        work = ctx.enter_context(tc.tile_pool(name="work", bufs=2))
        out_pool = ctx.enter_context(tc.tile_pool(name="o", bufs=OUT_TILES))
        tp_pool = ctx.enter_context(tc.psum_pool(name="tp", bufs=4))
        acc_pool = ctx.enter_context(tc.psum_pool(name="acc", bufs=4))

        ctx.enter_context(tc.manual_schedule())

        planes = const.tile([P, N_PASSES, D1], U8, align_bytes=64)
        nc.vector.memset(planes[:].rearrange("p w n -> p (w n)").bitcast(I32), 0)
        words = const.tile([P, N_PASSES, 2 * D1], U8, align_bytes=64)
        bias_bc = const.tile([P, D1], BF16)
        ident = const.tile([P, P], F32)
        make_identity(nc, ident[:])
        fours = const.tile([P, QUARTER], F32)
        nc.vector.tensor_reduce(
            out=fours[:], in_=ident[:].rearrange("p (w j) -> p w j", j=PER_SPIN), axis=mybir.AxisListType.X, op=ADD
        )
        averager = const.tile([P, QUARTER], BF16)
        nc.scalar.activation(out=averager[:], in_=fours[:], func=ACT.Copy, scale=1.0 / PER_SPIN)
        quarter = const.tile([P, P], BF16)
        nc.scalar.activation(out=quarter[:], in_=ident[:], func=ACT.Copy, scale=1.0 / PER_SPIN)
        ident_bf16 = const.tile([P, P], BF16)
        nc.vector.tensor_copy(out=ident_bf16[:], in_=ident[:])
        bias_col = const.tile([P, PACK], BF16)
        nc.gpsimd.dma_start(out=bias_col[:], in_=b_unmixed.rearrange("(p t) -> p t", t=PACK))

        def spread_bias():
            bias_bank = tp_pool.tile([P, PACK, P], BF16, tag="tp")
            for t in range(PACK):
                nc.tensor.transpose(bias_bank[:, t, :], bias_col[:, t : t + 1].to_broadcast([P, P]), ident_bf16[:])
            nc.scalar.copy(
                out=bias_bc[:].rearrange("p (k t) -> p k t", t=PACK), in_=bias_bank[:].rearrange("p t k -> p k t")
            )

        def weight_loads(place, w_words, w_scales):
            last = place + w_words.shape[0]
            loads = [(words[:, place:last, :].bitcast(I32), w_words.rearrange("g p n -> p g n").bitcast(I32))]
            for quad in range(4):
                rows = w_scales[:, 4 * quad : 4 * quad + 4, :].rearrange("g r n -> r g n")
                loads.append((planes[32 * quad : 32 * quad + 4, place:last, :].bitcast(I32), rows.bitcast(I32)))
            return loads

        def exchanged_weight_loads(place, w_words, w_scales):
            loads = []
            for h in range(2):
                rows = w_words[0, (1 - h) * HALF : (2 - h) * HALF, :]
                loads.append((words[h * HALF : (h + 1) * HALF, place, :].bitcast(I32), rows.bitcast(I32)))
            for quad in range(4):
                row = 4 * ((quad + 2) % 4)
                rows = w_scales[0, row : row + 4, :]
                loads.append((planes[32 * quad : 32 * quad + 4, place, :].bitcast(I32), rows.bitcast(I32)))
            return loads

        def block_and_electron(unit):
            return unit // UNITS_PER_BLOCK, PAIR * (unit % UNITS_PER_BLOCK)

        x1_of, e2_of, sums_of, grouped_of, codes_of, gb_of, acc_of, o_of = {}, {}, {}, {}, {}, {}, {}, {}

        def load_one_electron(blk):
            x1 = x1_pool.tile([P, SPINS * PER_SPIN, D1], BF16)
            nc.sync.dma_start(out=x1[:], in_=in_1e[blk * P : (blk + 1) * P])
            x1_of[blk] = x1

        def load_small(loads):
            for to, source in loads:
                nc.sync.dma_start(out=to, in_=source)

        def load_by_walker(unit):
            blk, electron = block_and_electron(unit)
            first = electron % PER_SPIN
            if first == 0:
                rows = ty_pool.tile([P, PER_SPIN, SPINS, PER_SPIN, D2], BF16, tag="ty")
                e2_of[unit // UNITS_PER_GROUP] = rows
            nc.sync.dma_start(
                out=e2_of[unit // UNITS_PER_GROUP][:, first : first + PAIR].rearrange("p i s j d -> p i (s j) d"),
                in_=in_2e[blk * P : (blk + 1) * P, electron : electron + PAIR],
            )

        def load_two_electron(g, between=()):
            blk, electron = block_and_electron(UNITS_PER_GROUP * g)
            ty = ty_pool.tile([P, PER_SPIN, PER_SPIN, SPINS, D2], BF16, tag="ty")
            all_partners = SPINS * PER_SPIN
            first_row, last_row = electron * all_partners, (electron + PER_SPIN) * all_partners - 1
            by_quarter = in_2e[blk * P : (blk + 1) * P].rearrange("(q w) i j d -> w q (i j) d", q=PER_SPIN)
            every_slot = ty[:].rearrange("p q i s d -> p q (i s) d")
            nc.sync.dma_start(out=every_slot[0:P:PER_SPIN, :, 0], in_=by_quarter[:, :, first_row])
            nc.sync.dma_start(out=every_slot[0:P:PER_SPIN, :, SPINS * PER_SPIN - 1], in_=by_quarter[:, :, last_row])
            for q in range(PER_SPIN):
                walkers = slice(blk * P + q * QUARTER, blk * P + (q + 1) * QUARTER)
                rows = in_2e[walkers].rearrange("w i j d -> w (i j) d")
                slots = ty[:, q].rearrange("p i s d -> p (i s) d")
                inner = rows[:, first_row + all_partners - 1 : last_row].rearrange("w (m r) d -> w m r d", r=all_partners)
                pairs = slots[0:P:PER_SPIN, 1 : SPINS * PER_SPIN - 1].rearrange("p (m r) d -> p m r d", r=SPINS)
                loads = [
                    (ty[1:P:PER_SPIN, q], in_2e[walkers, electron : electron + PER_SPIN, 1:all_partners:PER_SPIN, :]),
                    (ty[2:P:PER_SPIN, q], in_2e[walkers, electron : electron + PER_SPIN, 2:all_partners:PER_SPIN, :]),
                    (ty[3:P:PER_SPIN, q], in_2e[walkers, electron : electron + PER_SPIN, 3:5, :]),
                    (pairs, inner[:, :, 0:SPINS, :]),
                ]
                for number, (to, source) in enumerate(loads):
                    nc.sync.dma_start(out=to, in_=source)
                    if q * PER_SPIN + number < len(between):
                        load_small(between[q * PER_SPIN + number])
            e2_of[g] = ty

        def add_first_pairs(engine, blk, parts):
            if parts[0] == 0:
                m_half = work.tile([P, SPINS * 2, D1], F32, bufs=1)
                sums_of["half", blk] = m_half
            x1 = x1_of[blk]
            for part in parts:
                i = PER_SPIN * (part // 2) + part % 2
                engine.tensor_tensor(
                    out=sums_of["half", blk][:, part, :], in0=x1[:, i, :], in1=x1[:, i + 2, :], op=ADD
                )

        def add_second_pairs(blk):
            m_sum = work.tile([P, SPINS, D1], BF16, bufs=1)
            halves = sums_of["half", blk][:].rearrange("p (s l) d -> p s l d", l=2)
            nc.vector.tensor_tensor(out=m_sum[:], in0=halves[:, :, 0, :], in1=halves[:, :, 1, :], op=ADD)
            sums_of["m", blk] = m_sum

        def add_partners(unit):
            first = PAIR * (unit % UNITS_PER_GROUP)
            halves = e2_of[unit // UNITS_PER_GROUP][:, first : first + PAIR].rearrange("p i s (h l) d -> p (i s) h (l d)", h=2)
            a_half = work.tile([P, PAIR * SPINS, 2 * D2], F32, bufs=1)
            nc.vector.tensor_tensor(out=a_half[:], in0=halves[:, :, 0, :], in1=halves[:, :, 1, :], op=ADD)
            a_sum = work.tile([P, PAIR, SPINS * D2], BF16)
            rest = a_half[:].rearrange("p n (l d) -> p n l d", l=2)
            nc.vector.tensor_tensor(
                out=a_sum[:].rearrange("p i (s d) -> p (i s) d", s=SPINS),
                in0=rest[:, :, 0, :],
                in1=rest[:, :, 1, :],
                op=ADD,
            )
            sums_of["a", unit] = a_sum

        def transpose_rows(rows):
            as_words = rows.bitcast(F32)
            bank = tp_pool.tile([P, 2 * 2, P], F32, tag="tp")
            for r in range(2):
                for u in range(2):
                    nc.tensor.transpose(bank[:, 2 * r + u, :], as_words[:, r, u : D1 // 2 : 2], ident[:])
            return bank

        def average_two_electron(unit):
            first = PAIR * (unit % UNITS_PER_GROUP)
            features = e2_of[unit // UNITS_PER_GROUP][:].rearrange("p q i s d -> p q i (s d)")
            bank = tp_pool.tile([P, PAIR, PACK, P], BF16, tag="tp")
            for q in range(PER_SPIN):
                for e in range(PAIR):
                    for t in range(PACK):
                        nc.tensor.matmul(
                            out=bank[:, e, t, q * QUARTER : (q + 1) * QUARTER],
                            lhsT=features[:, q, first + e, t : SPINS * D2 : PACK],
                            rhs=averager[:],
                            start=True,
                            stop=True,
                        )
            nc.scalar.copy(out=grouped_of["xa", unit][:, PAIR:], in_=bank[:].rearrange("p e t w -> p e w t"))

        def transpose_inputs(unit):
            blk, electron = block_and_electron(unit)
            bank = transpose_rows(x1_of[blk][:, electron : electron + PAIR, :])
            xa_grouped = work.tile([P, 2 * PAIR, P, PACK], BF16, align_bytes=64, bufs=3)
            x_words = xa_grouped[:, 0:PAIR].rearrange("p i w t -> p (i w t)").bitcast(F32)
            x_words = x_words.rearrange("p (i w u) -> p i w u", i=PAIR, w=P, u=2)
            nc.scalar.copy(out=x_words, in_=bank[:].rearrange("p (r u) w -> p r w u", u=2))
            grouped_of["xa", unit] = xa_grouped

        def transpose_sums(sums, grouped):
            bank = transpose_rows(sums)
            values = bank[:].rearrange("p a w -> p (a w)").bitcast(BF16)
            values = values.rearrange("p (r u w e) -> p r w u e", r=2, u=2, w=P, e=2)
            for r in range(2):
                nc.scalar.activation(
                    out=grouped[:, r, :, :].rearrange("p w (u e) -> p w u e", u=2),
                    in_=values[:, r],
                    func=ACT.Copy,
                    scale=1.0 / PER_SPIN,
                )

        def transpose_one_electron_sums(blk):
            m_grouped = work.tile([P, SPINS, P, PACK], BF16, align_bytes=64, tag="m_grouped", bufs=1)
            transpose_sums(sums_of["m", blk][:], m_grouped)
            grouped_of["m", blk] = m_grouped

        def average_one_electron(blk):
            m_grouped = work.tile([P, SPINS, P, PACK], BF16, align_bytes=64, tag="m_grouped", bufs=1)
            for s in range(SPINS):
                bank = tp_pool.tile([P, PACK, P], F32, tag="tp")
                for t in range(PACK):
                    for i in range(PER_SPIN):
                        nc.tensor.matmul(
                            out=bank[:, t, :],
                            lhsT=x1_of[blk][:, PER_SPIN * s + i, t:D1:PACK],
                            rhs=quarter[:],
                            start=i == 0,
                            stop=i == PER_SPIN - 1,
                        )
                nc.scalar.copy(out=m_grouped[:, s], in_=bank[:].rearrange("p t w -> p w t"))
            grouped_of["m", blk] = m_grouped

        def quantise(key, count):
            grouped = grouped_of[key]
            bufs = 1 if key[0] == "m" else 2
            codes = work.tile([P, count, P], U32, align_bytes=64, tag="codes_" + key[0], bufs=bufs)
            scales = work.tile([P, count, P], U8, align_bytes=64, tag="scales_" + key[0], bufs=bufs)
            nc.vector.quantize_mx(
                out=codes[:].rearrange("p i w -> p (i w)").bitcast(FP8X4),
                scales=scales[:].rearrange("p i w -> p (i w)"),
                in_=grouped[:].rearrange("p i w t -> p (i w t)"),
            )
            codes_of[key] = (codes, scales)

        def quantise_unit(unit):
            quantise(("xa", unit), 2 * PAIR)

        def mx_pass(acc, key, row, place, start, stop):
            codes, scales = codes_of[key]
            nc.tensor.matmul_mx(
                out=acc[:],
                lhsT=codes[:, row, :].bitcast(FP8X4),
                lhsT_scale=scales[:, row, :],
                rhs=words[:, place, :].bitcast(FP4X4),
                rhs_scale=planes[:, place, :],
                start=start,
                stop=stop,
            )

        def multiply_means(blk):
            for s in range(SPINS):
                acc_g = acc_pool.tile([P, D1], F32, tag="acc")
                mx_pass(acc_g, ("m", blk), s, W_M_OWN, True, False)
                mx_pass(acc_g, ("m", blk), 1 - s, W_M_OTHER, False, True)
                acc_of["g", blk, s] = acc_g

        def add_bias(blk):
            gb = work.tile([P, SPINS, D1], F32)
            for s in range(SPINS):
                nc.vector.tensor_tensor(out=gb[:, s, :], in0=acc_of["g", blk, s][:], in1=bias_bc[:], op=ADD)
            gb_of[blk] = gb

        def multiply_unit(unit):
            blk, electron = block_and_electron(unit)
            for i in range(PAIR):
                acc = acc_pool.tile([P, D1], F32, tag="acc")
                mx_pass(acc, ("xa", unit), i, W_U, True, False)
                mx_pass(acc, ("xa", unit), PAIR + i, W_E + electron // PER_SPIN, False, True)
                acc_of[unit, i] = acc

        def leave_psum(unit):
            blk, electron = block_and_electron(unit)
            g, first = unit // UNITS_PER_GROUP, electron % PER_SPIN
            if first == 0:
                group_out = out_pool.tile([P, PER_SPIN, D1], F32)
                o_of["group", g] = group_out
            o = o_of["group", g][:, first : first + PAIR, :]
            for i in range(PAIR):
                nc.vector.tensor_tensor(
                    out=o[:, i, :], in0=acc_of[unit, i][:], in1=gb_of[blk][:, electron // PER_SPIN, :], op=ADD
                )
                if unit == LAST:
                    nc.scalar.activation(out=o[:, i, :], in_=o[:, i, :], func=ACT.Tanh)
            if unit != LAST:
                nc.scalar.activation(out=o, in_=o, func=ACT.Tanh)
            o_of[unit] = o

        def store_unit(unit):
            blk, electron = block_and_electron(unit)
            g = unit // UNITS_PER_GROUP
            walkers = slice(blk * P, (blk + 1) * P)
            if unit == LAST:
                for i in range(PAIR):
                    nc.sync.dma_start(out=out[walkers, electron + i, :], in_=o_of[unit][:, i, :])
            elif g == GROUPS - 1:
                nc.sync.dma_start(out=out[walkers, electron : electron + PAIR, :], in_=o_of[unit])
            elif electron % PER_SPIN:
                first = electron - PAIR
                nc.sync.dma_start(out=out[walkers, first : first + PER_SPIN, :], in_=o_of["group", g][:])

        def finish_unit(unit):
            blk, electron = block_and_electron(unit)
            o = o_of[unit]
            x1 = x1_of[blk][:, electron : electron + PAIR, :]
            if unit == LAST:
                for i in range(PAIR):
                    nc.vector.tensor_tensor(out=o[:, i, :], in0=o[:, i, :], in1=x1[:, i, :], op=ADD)
            else:
                nc.vector.tensor_tensor(out=o, in0=o, in1=x1, op=ADD)


        def by_walker(unit):
            return unit // UNITS_PER_GROUP in WALKER_GROUPS

        def load_group(g, between=()):
            if g in WALKER_GROUPS:
                for unit in range(UNITS_PER_GROUP * g, UNITS_PER_GROUP * (g + 1)):
                    load_by_walker(unit)
            else:
                load_two_electron(g, between)
            if g % SPINS == 0 and g and g // SPINS + 1 < BLOCKS:
                load_one_electron(g // SPINS + 1)

        def is_unit(unit):
            return 0 <= unit < UNITS

        def sparse(loads, every):
            out_list = []
            for load in loads:
                out_list += [()] * (every - 1) + [(load,)]
            return out_list

        load_by_walker(0)
        load_one_electron(0)
        load_small(weight_loads(W_M_OWN, wm_words, wm_scales))
        load_by_walker(1)
        load_small(weight_loads(W_U, wu_words, wu_scales))
        load_by_walker(2)
        load_small(weight_loads(W_E, w2_words, w2_scales))
        load_by_walker(3)
        load_small(exchanged_weight_loads(W_E + 1, w2_words, w2_scales))
        load_one_electron(1)
        for g in range(2, GROUPS_AHEAD):
            load_group(g)
        def block_at(n, offset):
            first = n + offset
            if first % UNITS_PER_BLOCK == 0 and 0 <= first // UNITS_PER_BLOCK < BLOCKS:
                return first // UNITS_PER_BLOCK
            return None
        finished = []
        for n in range(-2, UNITS + 3):
            if is_unit(n + 1):
                transpose_inputs(n + 1)
            if n == -2:
                average_one_electron(0)
            b = block_at(n, 1)
            if b:
                transpose_one_electron_sums(b)
            if n == 0:
                spread_bias()
            b = block_at(n, 0)
            if b is not None:
                quantise(("m", b), SPINS)
            if is_unit(n - 1):
                quantise_unit(n - 1)
            b = block_at(n, -1)
            if b is not None:
                add_bias(b)
            if is_unit(n - 2):
                leave_psum(n - 2)
            if is_unit(n - 1):
                multiply_unit(n - 1)
            b = block_at(n, 0)
            if b is not None:
                multiply_means(b)
            if is_unit(n - 3):
                finish_unit(n - 3)
                finished.append(n - 3)
            b = block_at(n, 2)
            if b:
                add_second_pairs(b)
            if n >= -2:
                b = (n + 6) // UNITS_PER_BLOCK
                if 1 <= b < BLOCKS:
                    add_first_pairs(nc.gpsimd, b, [(n + 2) % UNITS_PER_BLOCK])
            if is_unit(n + 2) and by_walker(n + 2):
                add_partners(n + 2)
            if is_unit(n + 1):
                if by_walker(n + 1):
                    transpose_sums(sums_of["a", n + 1][:], grouped_of["xa", n + 1][:, PAIR:])
                else:
                    average_two_electron(n + 1)
            ahead = n // UNITS_PER_GROUP + GROUPS_AHEAD
            if n >= 0 and n % UNITS_PER_GROUP == 0 and ahead < GROUPS:
                load_group(ahead)
            while finished and n >= UNITS_PER_GROUP * (GROUPS - 1 - GROUPS_AHEAD):
                store_unit(finished.pop(0))
